import numpy as np
import ml_dtypes


def mxq(x, axis, fmt="e4m3"):
    dtype, down = {"e4m3": (ml_dtypes.float8_e4m3fn, 7), "e5m2": (ml_dtypes.float8_e5m2, 14)}[fmt]
    v = np.moveaxis(np.asarray(x, np.float32).astype(ml_dtypes.bfloat16).astype(np.float64), axis, -1)
    blocks = v.reshape(v.shape[:-1] + (-1, 32))
    amax = np.abs(blocks).max(-1, keepdims=True)
    byte = np.maximum(np.where(amax > 0, np.frexp(amax)[1] - 1 + 127, 0) - down, 1)
    scale = np.exp2(byte - 127.0)
    codes = (blocks / scale).astype(np.float32).astype(dtype).astype(np.float64)
    return np.moveaxis((codes * scale).reshape(v.shape), -1, axis)


WIDE = False


def mx_kscale(k):
    if not WIDE:
        return np.ones(k)
    levels = np.array([30, -30])
    if k % 512:
        return np.exp2(np.random.permutation(np.resize(levels, k // 32))).repeat(32)
    a = np.empty((k // 512, 16))
    for p in range(k // 512):
        a[p, :8] = np.random.permutation(np.resize(levels, 8))
        for g in range(8):
            far = levels[np.abs(levels - a[p, g]) >= 10]
            a[p, g + 8] = far[np.random.randint(len(far))]
    return np.exp2(a.ravel()).repeat(32)


BF16 = ml_dtypes.bfloat16


def bf(x):
    return np.asarray(x, np.float32).astype(BF16)


def f64(x):
    return np.asarray(x).astype(np.float64)


B, IN, H = 2048, 512, 512
G = 4 * H
EPS = 1e-5


def _layernorm(v, gamma, beta):
    mean = np.mean(v, axis=-1, keepdims=True)
    var = np.mean(np.square(v - mean), axis=-1, keepdims=True)
    return (v - mean) / np.sqrt(var + EPS) * gamma + beta


def sigmoid(v):
    return 1.0 / (1.0 + np.exp(-v))


def setup_inputs():
    s, t = mx_kscale(IN), mx_kscale(H)
    return {
        "x": bf(np.random.standard_normal((B, IN)) * s),
        "h_prev": bf(np.random.standard_normal((B, H)) * t),
        "c_prev": bf(np.random.standard_normal((B, H))),
        "W_ih": bf(np.random.standard_normal((IN, G)) / np.sqrt(IN) / s[:, None]),
        "W_hh": bf(np.random.standard_normal((H, G)) / np.sqrt(H) / t[:, None]),
        "gamma_ih": bf(1.0 + 0.2 * np.random.standard_normal(G)),
        "beta_ih": bf(0.3 * np.random.standard_normal(G)),
        "gamma_hh": bf(1.0 + 0.2 * np.random.standard_normal(G)),
        "beta_hh": bf(0.3 * np.random.standard_normal(G)),
        "gamma_c": bf(1.0 + 0.2 * np.random.standard_normal(H)),
        "beta_c": bf(0.3 * np.random.standard_normal(H)),
    }


def reference(x, h_prev, c_prev, W_ih, W_hh, gamma_ih, beta_ih, gamma_hh, beta_hh, gamma_c, beta_c):
    a_ih = mxq(f64(x), 1, "e5m2") @ mxq(f64(W_ih), 0, "e5m2")
    a_hh = mxq(f64(h_prev), 1, "e5m2") @ mxq(f64(W_hh), 0, "e5m2")
    gates_ih = _layernorm(a_ih, f64(gamma_ih), f64(beta_ih))
    gates_hh = _layernorm(a_hh, f64(gamma_hh), f64(beta_hh))
    gates = gates_ih + gates_hh
    i_g, f_g, g_g, o_g = np.split(gates, 4, axis=1)
    i_t = sigmoid(i_g)
    f_t = sigmoid(f_g)
    g_t = np.tanh(g_g)
    o_t = sigmoid(o_g)
    c_t = f_t * f64(c_prev) + i_t * g_t
    h_t = o_t * np.tanh(_layernorm(c_t, f64(gamma_c), f64(beta_c)))
    return (h_t, c_t)

@@ -1,0 +1,608 @@
+from contextlib import ExitStack
+
+import concourse.mybir as mybir
+from concourse.masks import make_identity
+
+B, K, H = 2048, 512, 512
+G = 4 * H
+EPS = 1e-5
+FLOPS = 2 * 2 * B * K * G
+
+F32 = mybir.dt.float32
+BF16 = mybir.dt.bfloat16
+U32 = mybir.dt.uint32
+U8 = mybir.dt.uint8
+FP8X4 = mybir.dt.float8_e5m2_x4
+ALU = mybir.AluOpType
+ACT = mybir.ActivationFunctionType
+
+P = 128
+PACK = 4
+BANK = 512
+TILES = 2
+LOAD_TILES = 4
+ROWS = TILES * P
+PER_BANK = BANK // ROWS
+GROUPS = B // (P * TILES)
+CHUNKS = G // BANK
+GATE_I, GATE_F, GATE_G, GATE_O = 0, 1, 2, 3
+TURNED_GATES = (GATE_I, GATE_G, GATE_F)
+STEPS = len(TURNED_GATES) * TILES
+PAIRS = 2 * TILES
+SCALAR_PAIRS = (2, 1, 2, 1, 2, 1, 2, 1)
+FIRST = 1
+CHAIN = 3
+UB = 5
+EXTRA = 2
+VEC_FROM = 7
+HV = 1
+HEAD_CHUNKS = 8
+NORM_IN_PSUM = True
+C0 = 0
+C1 = 1
+C2 = 2
+C3 = 3
+C4 = 5
+C5 = 6
+VB = 4
+SB = 3
+SUM_LAG = 2
+CELL_GAP = 3
+LAST_CELL_GAP = 1
+
+
+def tile_layernormlstmcell_kernel(
+    tc, x, h_prev, c_prev, W_ih, W_hh, gamma_ih, beta_ih, gamma_hh, beta_hh, gamma_c, beta_c, out_0, out_1
+):
+    nc = tc.nc
+    acts = (x, h_prev)
+    weights = (W_ih, W_hh)
+
+    with ExitStack() as ctx:
+        keep = ctx.enter_context(tc.tile_pool(name="keep", bufs=1))
+        work = ctx.enter_context(tc.tile_pool(name="work", bufs=2))
+        psum = ctx.enter_context(tc.psum_pool(name="psum", bufs=4))
+        ctx.enter_context(tc.manual_schedule())
+
+        def vector_bank():
+            return psum.tile([P, BANK], F32, name="vector_bank", tag="vector_bank", bufs=VB)
+
+        def scalar_bank(dtype=F32):
+            return psum.tile([P, BANK], dtype, name="scalar_bank", tag="scalar_bank", bufs=SB)
+
+        ident = keep.tile([P, P], F32, name="ident")
+        ident_bf = keep.tile([P, P], BF16, name="ident_bf")
+        w_codes = [keep.tile([P, G], U32, name="w_codes%d" % m, align_bytes=64) for m in range(2)]
+        w_scales = [keep.tile([P, G], U8, name="w_scales%d" % m, align_bytes=64) for m in range(2)]
+        gamma_rows = keep.tile([P, P], BF16, name="gamma_rows")
+        gamma_cols = keep.tile([P, 2 * G // P], F32, name="gamma_cols")
+        shift_rhs = keep.tile([P, GATE_O * H], BF16, name="shift_rhs")
+        pieces = [keep.tile([P, TILES, P], BF16, name="pieces%d" % i) for i in range(2)]
+        gamma_o = [keep.tile([P, H], BF16, name="gamma_o%d" % m) for m in range(2)]
+        beta_o_parts = [keep.tile([P, H], BF16, name="beta_o_part%d" % m) for m in range(2)]
+        beta_o = keep.tile([P, H], F32, name="beta_o")
+        if NORM_IN_PSUM:
+            norm_c = psum.tile([P, 2 * H], BF16, name="norm_c", bufs=1)
+            norm_cols = keep.tile([P, 8], BF16, name="norm_cols")
+        else:
+            norm_c = keep.tile([P, 2 * H], BF16, name="norm_c")
+        gamma_c_all, beta_c_all = norm_c[:, :H], norm_c[:, H:]
+        minus_half = keep.tile([P, PAIRS], F32, name="minus_half")
+
+        st = {}
+
+        def load_rows(key, src, g, tag, bufs):
+            raw = work.tile([P, LOAD_TILES, K], BF16, name=tag, tag=tag, bufs=bufs)
+            rows = src[g * LOAD_TILES * P : (g + 1) * LOAD_TILES * P, :]
+            nc.sync.dma_start(out=raw[:], in_=rows.rearrange("(t p) k -> p t k", p=P))
+            st[key, g] = raw
+
+        def load_act(m, g):
+            load_rows(("raw", m), acts[m], g, "raw", 6)
+
+        def load_weight(m, c):
+            raw = work.tile([P, PACK, BANK], BF16, name="raw", tag="raw", bufs=6)
+            cols = weights[m][:, c * BANK : (c + 1) * BANK]
+            nc.sync.dma_start(out=raw[:], in_=cols.rearrange("(p j) n -> p j n", j=PACK))
+            st["w_raw", m, c] = raw
+
+        def grouped_tile():
+            return work.tile([P, BANK * PACK], BF16, name="grouped", tag="grouped", bufs=3, align_bytes=64)
+
+        def interleave_weight(m, c, copy):
+            grouped = grouped_tile()
+            copy(
+                out=grouped[:].rearrange("p (c i j) -> p c j i", i=4, j=PACK),
+                in_=st["w_raw", m, c][:].rearrange("p j (c i) -> p c j i", i=4),
+            )
+            st["w_grouped", m, c] = grouped
+
+        def quantize_weight(m, c):
+            cols = slice(c * BANK, (c + 1) * BANK)
+            nc.vector.quantize_mx(
+                out=w_codes[m][:, cols].bitcast(FP8X4), scales=w_scales[m][:, cols], in_=st["w_grouped", m, c][:]
+            )
+
+        def turn_act(m, g, half):
+            if half == 0:
+                st["grouped", m, g] = grouped_tile()
+            bank = scalar_bank()
+            for i in range(2):
+                words = st[("raw", m), g][:, 2 * half + i, :].bitcast(F32)
+                for u in range(2):
+                    at = (2 * i + u) * P
+                    nc.tensor.transpose(bank[:, at : at + P], words[:, u : K // 2 : 2], ident[:])
+            dst = st["grouped", m, g][:].bitcast(F32)[:, half * BANK : (half + 1) * BANK]
+            nc.scalar.copy(
+                out=dst.rearrange("p (i r u) -> p i r u", i=2, u=2),
+                in_=bank[:].rearrange("p (i u r) -> p i r u", i=2, u=2),
+            )
+
+        def quantize_act(m, g):
+            codes = work.tile([P, BANK], U32, name="a_codes%d" % m, bufs=3, align_bytes=64)
+            scales = work.tile([P, BANK], U8, name="a_scales%d" % m, bufs=3, align_bytes=64)
+            nc.vector.quantize_mx(out=codes[:].bitcast(FP8X4), scales=scales[:], in_=st["grouped", m, g][:])
+            st["codes", m, g] = (codes, scales)
+
+        def product_rows(bank, m, g, t, c):
+            codes, scales = st["codes", m, g // 2]
+            t += g % 2 * TILES
+            rows, cols = slice(t * P, (t + 1) * P), slice(c * BANK, (c + 1) * BANK)
+            nc.tensor.matmul_mx(
+                out=bank[:],
+                lhsT=codes[:, rows].bitcast(FP8X4),
+                lhsT_scale=scales[:, rows],
+                rhs=w_codes[m][:, cols].bitcast(FP8X4),
+                rhs_scale=w_scales[m][:, cols],
+                start=True,
+                stop=True,
+            )
+
+        def product_channels(bank, m, g, j):
+            codes, scales = st["codes", m, g // 2]
+            cols = slice(j * P, (j + 1) * P)
+            rows = slice(g % 2 * ROWS, (g % 2 + 1) * ROWS)
+            nc.tensor.matmul_mx(
+                out=bank,
+                lhsT=w_codes[m][:, cols].bitcast(FP8X4),
+                lhsT_scale=w_scales[m][:, cols],
+                rhs=codes[:, rows].bitcast(FP8X4),
+                rhs_scale=scales[:, rows],
+                start=True,
+                stop=True,
+            )
+
+        def open_stats(g):
+            st["mean_var", g] = work.tile([P, PAIRS, 2], F32, name="mean_var", bufs=4)
+            st["squares", g] = work.tile([P, 2, TILES], F32, name="squares", bufs=3)
+
+        def vector_stats(g, pair, c):
+            if c == 0:
+                st["bn", g, pair] = work.tile([P, CHUNKS, 6], F32, name="bn", bufs=PAIRS)
+            bank = vector_bank()
+            product_rows(bank, pair // TILES, g, pair % TILES, c)
+            nc.vector.bn_stats(out=st["bn", g, pair][:, c, :], in_=bank[:])
+
+        def vector_stats_end(g, pair):
+            nc.vector.bn_aggr(out=st["mean_var", g][:, pair, :], in_=st["bn", g, pair][:].rearrange("p c s -> p (c s)"))
+
+        def scalar_sum(g, pair, c):
+            if c == 0:
+                st["scaled", g, pair] = work.tile([P, G], F32, name="scaled", bufs=2)
+                st["part", g, pair] = work.tile([P, 2, CHUNKS], F32, name="part", bufs=3)
+            bank = scalar_bank()
+            product_rows(bank, pair // TILES, g, pair % TILES, c)
+            nc.scalar.activation(
+                out=st["scaled", g, pair][:, c * BANK : (c + 1) * BANK],
+                in_=bank[:],
+                func=ACT.Copy,
+                scale=1.0 / G,
+                accum_out=st["part", g, pair][:, 0, c : c + 1],
+            )
+
+        def scalar_mean(g, pair):
+            part = st["part", g, pair]
+            nc.scalar.activation(
+                out=part[:, 1, :], in_=part[:, 0, :], func=ACT.Copy, accum_out=st["mean_var", g][:, pair, 0:1]
+            )
+
+        def scalar_squares(g, pair, half):
+            scaled = st["scaled", g, pair][:, half * G // 2 : (half + 1) * G // 2]
+            at = pair - TILES
+            nc.scalar.activation(
+                out=scaled,
+                in_=scaled,
+                func=ACT.Square,
+                scale=-float(G),
+                bias=st["mean_var", g][:, pair, 0:1],
+                accum_out=st["squares", g][:, half, at : at + 1],
+            )
+
+        def row_rstd(g):
+            mean_var, squares = st["mean_var", g], st["squares", g]
+            first = PAIRS - SCALAR_PAIRS[g]
+            var_eps = work.tile([P, PAIRS], F32, name="var_eps", bufs=3)
+            rstd = work.tile([P, PAIRS], F32, name="rstd", bufs=3)
+            minus_mean = work.tile([P, PAIRS], F32, name="minus_mean", bufs=3)
+            low, high = squares[:, 0, first - TILES :], squares[:, 1, first - TILES :]
+            nc.gpsimd.tensor_tensor(low, low, high, ALU.add)
+            nc.gpsimd.tensor_scalar(var_eps[:, :first], mean_var[:, :first, 1], 1.0, EPS, ALU.mult, ALU.add)
+            nc.gpsimd.tensor_scalar(var_eps[:, first:], low, 1.0 / G, EPS, ALU.mult, ALU.add)
+            nc.gpsimd.tensor_tensor(rstd[:], var_eps[:], minus_half[:], ALU.pow)
+            nc.gpsimd.tensor_scalar(minus_mean[:], mean_var[:, :, 0], -1.0, 0.0, ALU.mult, ALU.add)
+            st["rstd", g], st["var_eps", g], st["minus_mean", g] = rstd, var_eps, minus_mean
+
+        def row_terms(g):
+            rstd, var_eps, minus_mean = st["rstd", g], st["var_eps", g], st["minus_mean", g]
+            terms = work.tile([P, TILES, 4], F32, name="terms", bufs=3)
+            ratio = work.tile([P, TILES], F32, name="ratio", bufs=3)
+            nc.gpsimd.tensor_tensor(terms[:, :, 0], var_eps[:, :TILES], rstd[:, :TILES], ALU.mult)
+            nc.gpsimd.tensor_tensor(terms[:, :, 1], var_eps[:, :TILES], rstd[:, :TILES], ALU.mult)
+            nc.gpsimd.tensor_tensor(ratio[:], terms[:, :, 0], rstd[:, TILES:], ALU.mult)
+            nc.gpsimd.tensor_copy(out=terms[:, :, 2], in_=minus_mean[:, :TILES])
+            nc.gpsimd.tensor_tensor(terms[:, :, 3], minus_mean[:, TILES:], ratio[:], ALU.mult)
+            st["terms", g], st["ratio", g] = terms, ratio
+
+        def row_pieces(g):
+            terms = st["terms", g]
+            rest = work.tile([P, TILES, 4], F32, name="rest", bufs=3)
+            split = pieces[g % 2][:, :, 0:12].rearrange("p t (v s) -> p t v s", s=3)
+            nc.gpsimd.tensor_copy(out=split[:, :, :, 0], in_=terms[:])
+            nc.gpsimd.tensor_tensor(rest[:], terms[:], split[:, :, :, 0], ALU.subtract)
+            nc.gpsimd.tensor_copy(out=split[:, :, :, 1], in_=rest[:])
+            nc.gpsimd.tensor_tensor(rest[:], rest[:], split[:, :, :, 1], ALU.subtract)
+            nc.gpsimd.tensor_copy(out=split[:, :, :, 2], in_=rest[:])
+
+        def spread_ratio(g):
+            bank = scalar_bank()
+            for t in range(TILES):
+                col = st["ratio", g][:, t : t + 1].to_broadcast([P, P])
+                nc.tensor.transpose(bank[:, t * P : (t + 1) * P], col, ident[:])
+            ratio_all = work.tile([P, ROWS], F32, name="ratio_all")
+            nc.scalar.copy(out=ratio_all[:], in_=bank[:, :ROWS])
+            st["ratio_all", g] = ratio_all
+
+        def turn_pieces(g):
+            bank = scalar_bank(BF16)
+            for t in range(TILES):
+                nc.tensor.transpose(bank[:, t * P : (t + 1) * P], pieces[g % 2][:, t, :], ident_bf[:])
+            shift_lhs = work.tile([P, ROWS], BF16, name="shift_lhs")
+            nc.scalar.copy(out=shift_lhs[:], in_=bank[:, :ROWS])
+            st["shift_lhs", g] = shift_lhs
+
+        def channel_block(s, i):
+            n = s * PER_BANK + i
+            return TURNED_GATES[n // 4] * 4 + n % 4
+
+        def scaled_ih(g, s):
+            bank = scalar_bank()
+            u = work.tile([P, PER_BANK, ROWS], F32, name="u_ih", bufs=UB)
+            for i in range(PER_BANK):
+                product_channels(bank[:, i * ROWS : (i + 1) * ROWS], 0, g, channel_block(s, i))
+            for i in range(PER_BANK):
+                j = channel_block(s, i)
+                nc.scalar.activation(
+                    out=u[:, i, :], in_=bank[:, i * ROWS : (i + 1) * ROWS], func=ACT.Copy, scale=gamma_cols[:, j : j + 1]
+                )
+            st["u", 0, g, s] = u
+
+        def scaled_hh(g, s):
+            bank = vector_bank()
+            u = work.tile([P, PER_BANK, ROWS], F32, name="u_hh", bufs=UB)
+            for i in range(PER_BANK):
+                product_channels(bank[:, i * ROWS : (i + 1) * ROWS], 1, g, channel_block(s, i))
+            for i in range(PER_BANK):
+                j = G // P + channel_block(s, i)
+                nc.vector.scalar_tensor_tensor(
+                    u[:, i, :],
+                    bank[:, i * ROWS : (i + 1) * ROWS],
+                    gamma_cols[:, j : j + 1],
+                    st["ratio_all", g][:],
+                    ALU.mult,
+                    ALU.mult,
+                )
+            st["u", 1, g, s] = u
+
+        def gate(g, item):
+            q, t = divmod(item, TILES)
+            which = TURNED_GATES[q]
+            rows = slice(t * P, (t + 1) * P)
+            bank = scalar_bank()
+            nc.tensor.matmul(
+                bank[:], st["shift_lhs", g][:, rows], shift_rhs[:, which * H : (which + 1) * H], start=True, stop=False
+            )
+            for m in range(2):
+                for i in range(4):
+                    nc.tensor.matmul(
+                        bank[:, i * P : (i + 1) * P],
+                        st["u", m, g, (4 * q + i) // PER_BANK][:, i % PER_BANK, rows],
+                        ident[:],
+                        start=False,
+                        stop=(m == 1 and i == 3),
+                        is_transpose=True,
+                    )
+            value = work.tile([P, H], F32, name="gate%d" % which, bufs=4)
+            func = ACT.Tanh if which == GATE_G else ACT.Sigmoid
+            nc.scalar.activation(out=value[:], in_=bank[:], func=func, scale=st["rstd", g][:, t : t + 1])
+            st["gate", which, g, t] = value
+
+        def o_centred(g, t, m):
+            bank = vector_bank()
+            product_rows(bank, m, g, t, GATE_O)
+            u = work.tile([P, H], F32, name="o_part%d" % m, bufs=2 + 2 * m)
+            mean = st["mean_var", g][:, m * TILES + t, 0:1]
+            nc.vector.scalar_tensor_tensor(u[:], bank[:], mean, gamma_o[m][:], ALU.subtract, ALU.mult)
+            st["o_part", m, g, t] = u
+
+        def o_sum(g, t):
+            u = st["o_part", 1, g, t]
+            ratio = st["ratio", g][:, t : t + 1]
+            nc.vector.scalar_tensor_tensor(u[:], u[:], ratio, st["o_part", 0, g, t][:], ALU.mult, ALU.add)
+
+        def o_bias(g, t):
+            u = st["o_part", 1, g, t]
+            nc.vector.scalar_tensor_tensor(u[:], beta_o[:], st["terms", g][:, t, 0:1], u[:], ALU.mult, ALU.add)
+
+        def o_gate(g, t):
+            value = work.tile([P, H], F32, name="gate_o", bufs=6)
+            nc.scalar.activation(
+                out=value[:], in_=st["o_part", 1, g, t][:], func=ACT.Sigmoid, scale=st["rstd", g][:, t : t + 1]
+            )
+            st["gate", GATE_O, g, t] = value
+
+        def input_term(g, t):
+            i_gate = st["gate", GATE_I, g, t]
+            nc.gpsimd.tensor_tensor(i_gate[:], i_gate[:], st["gate", GATE_G, g, t][:], ALU.mult)
+            st["input_term", g, t] = i_gate
+
+        def cell(g, t):
+            f_gate = st["gate", GATE_F, g, t]
+            c_new = work.tile([P, H], F32, name="c_new", bufs=3)
+            engine = nc.vector if g >= VEC_FROM else nc.gpsimd
+            engine.tensor_tensor(f_gate[:], f_gate[:], st["c_prev", g // 2][:, g % 2 * TILES + t, :], ALU.mult)
+            st["c", g, t] = c_new
+
+        def cell_sum(g, t):
+            f_gate = st["gate", GATE_F, g, t]
+            c_new = st["c", g, t]
+            engine = nc.vector if g >= VEC_FROM else nc.gpsimd
+            engine.tensor_tensor(c_new[:], f_gate[:], st["input_term", g, t][:], ALU.add)
+            row = (g * TILES + t) * P
+            nc.sync.dma_start(out=out_1[row : row + P, :], in_=c_new[:])
+
+        def cell_stats(g, t):
+            bn = work.tile([P, 6], F32, name="c_bn")
+            nc.vector.bn_stats(out=bn[:], in_=st["c", g, t][:])
+            st["c_bn", g, t] = bn
+
+        def cell_mean(g, t):
+            mean_var = work.tile([P, 2], F32, name="c_mean_var", bufs=3)
+            nc.vector.bn_aggr(out=mean_var[:], in_=st["c_bn", g, t][:])
+            st["c_mean", g, t] = mean_var
+
+        def cell_rstd(g, t):
+            mean_var = st["c_mean", g, t]
+            var_eps = work.tile([P, 1], F32, name="c_var_eps", bufs=3)
+            rstd = work.tile([P, 1], F32, name="c_rstd", bufs=3)
+            nc.gpsimd.tensor_scalar(var_eps[:], mean_var[:, 1:2], 1.0, EPS, ALU.mult, ALU.add)
+            nc.gpsimd.tensor_tensor(rstd[:], var_eps[:], minus_half[:, 0:1], ALU.pow)
+            st["c_rstd", g, t] = rstd
+
+        def cell_centred(g, t):
+            y = work.tile([P, H], F32, name="c_norm", bufs=4)
+            mean = st["c_mean", g, t][:, 0:1]
+            nc.vector.scalar_tensor_tensor(y[:], st["c", g, t][:], mean, gamma_c_all, ALU.subtract, ALU.mult)
+            st["c_norm", g, t] = y
+
+        def cell_bias(g, t):
+            y = st["c_norm", g, t]
+            nc.vector.scalar_tensor_tensor(y[:], y[:], st["c_rstd", g, t][:], beta_c_all, ALU.mult, ALU.add)
+
+        def cell_tanh(g, t):
+            y = st["c_norm", g, t]
+            nc.scalar.activation(out=y[:], in_=y[:], func=ACT.Tanh)
+
+        def hidden(g, t):
+            y = st["c_norm", g, t]
+            h_new = work.tile([P, H], F32, name="h_new")
+            engine = nc.vector if g == GROUPS - 1 and t % 2 == 1 else nc.gpsimd
+            engine.tensor_tensor(h_new[:], y[:], st["gate", GATE_O, g, t][:], ALU.mult)
+            row = (g * TILES + t) * P
+            nc.sync.dma_start(out=out_0[row : row + P, :], in_=h_new[:])
+
+        def pool_copy(out, in_):
+            nc.gpsimd.tensor_scalar(out, in_, 1.0, 0.0, ALU.mult, ALU.add)
+
+        def vector_pairs(g):
+            return list(range(PAIRS - SCALAR_PAIRS[g]))
+
+        def scalar_pairs(g):
+            return list(range(PAIRS - SCALAR_PAIRS[g], PAIRS))
+
+        load_act(0, 0)
+        load_weight(0, 0)
+        load_weight(0, 1)
+        load_weight(0, 2)
+        load_weight(0, 3)
+        load_act(1, 0)
+        make_identity(nc, ident[:])
+        make_identity(nc, ident_bf[:])
+        nc.gpsimd.memset(gamma_rows[:], 0.0)
+        nc.gpsimd.memset(shift_rhs[:], 0.0)
+        nc.gpsimd.memset(minus_half[:], -0.5)
+        for i in range(2):
+            nc.gpsimd.memset(pieces[i][:], 0.0)
+        open_stats(0)
+        turn_act(0, 0, 0)
+        turn_act(0, 0, 1)
+        load_weight(1, 0)
+        interleave_weight(0, 0, nc.vector.tensor_copy)
+        load_weight(1, 1)
+        quantize_act(0, 0)
+        interleave_weight(0, 1, nc.scalar.copy)
+        quantize_weight(0, 0)
+        load_weight(1, 2)
+        interleave_weight(0, 2, nc.vector.tensor_copy)
+        load_weight(1, 3)
+        quantize_weight(0, 1)
+        interleave_weight(0, 3, nc.vector.tensor_copy)
+        load_act(0, 1)
+        quantize_weight(0, 2)
+        turn_act(1, 0, 0)
+        turn_act(1, 0, 1)
+        load_act(1, 1)
+        vector_stats(0, 0, 0)
+        quantize_weight(0, 3)
+        interleave_weight(1, 0, nc.scalar.copy)
+        vector_stats(0, 0, 1)
+        quantize_act(1, 0)
+        interleave_weight(1, 1, nc.vector.tensor_copy)
+        vector_stats(0, 0, 2)
+        quantize_weight(1, 0)
+        interleave_weight(1, 2, nc.scalar.copy)
+        vector_stats(0, 0, 3)
+        quantize_weight(1, 1)
+        interleave_weight(1, 3, nc.vector.tensor_copy)
+        vector_stats(0, 1, 0)
+        quantize_weight(1, 2)
+        vector_stats(0, 1, 1)
+        quantize_weight(1, 3)
+        for m, gamma in enumerate((gamma_ih, gamma_hh)):
+            nc.sync.dma_start(
+                out=gamma_rows[m * G // P : (m + 1) * G // P, :], in_=gamma.rearrange("(j n) -> j n", n=P)
+            )
+        if NORM_IN_PSUM:
+            for m, vec in enumerate((gamma_c, beta_c)):
+                nc.sync.dma_start(out=gamma_rows[32 + 4 * m : 36 + 4 * m, :], in_=vec.rearrange("(j n) -> j n", n=P))
+        for v, vec in enumerate((beta_ih, beta_hh, gamma_ih, gamma_hh)):
+            nc.sync.dma_start(out=shift_rhs[3 * v : 3 * v + 3, :], in_=vec[: GATE_O * H].partition_broadcast(3))
+        for dst, vec in zip(gamma_o + beta_o_parts, (gamma_ih, gamma_hh, beta_ih, beta_hh)):
+            nc.sync.dma_start(out=dst[:], in_=vec[GATE_O * H :].partition_broadcast(P))
+        if not NORM_IN_PSUM:
+            nc.sync.dma_start(out=gamma_c_all, in_=gamma_c.partition_broadcast(P))
+            nc.sync.dma_start(out=beta_c_all, in_=beta_c.partition_broadcast(P))
+
+        vector_list = [(0, pair, c) for pair in vector_pairs(0) for c in range(CHUNKS)][6:]
+        vector_list += [(1, pair, c) for pair in vector_pairs(1) for c in range(CHUNKS)][:HEAD_CHUNKS]
+        scalar_list = []
+        for g, pair in [(0, pair) for pair in scalar_pairs(0)] + [(1, scalar_pairs(1)[0])]:
+            scalar_list += [(scalar_sum, g, pair, c) for c in range(CHUNKS)]
+            scalar_list += [(scalar_mean, g, pair)]
+            scalar_list += [(scalar_squares, g, pair, 0), (scalar_squares, g, pair, 1)]
+            if g == 0 and pair == scalar_pairs(0)[-1]:
+                scalar_list += [(row_rstd, 0), (row_terms, 0), (row_pieces, 0)]
+        open_stats(1)
+        vector_stats_end(0, 0)
+        nc.gpsimd.tensor_tensor(beta_o[:], beta_o_parts[0][:], beta_o_parts[1][:], ALU.add)
+        taken = 0
+        for n, entry in enumerate(scalar_list):
+            entry[0](*entry[1:])
+            while taken < len(vector_list) * (n + 1) // len(scalar_list):
+                g, pair, c = vector_list[taken]
+                taken += 1
+                vector_stats(g, pair, c)
+                if c == 0 and taken > 2:
+                    vector_stats_end(*vector_list[taken - 2][:2])
+        if HEAD_CHUNKS % CHUNKS == 0:
+            vector_stats_end(*vector_list[-1][:2])
+        for m in range(2):
+            turn_act(m, 1, 0)
+            turn_act(m, 1, 1)
+            quantize_act(m, 1)
+        bank = scalar_bank(BF16)
+        nc.tensor.transpose(bank[:, :P], gamma_rows[:], ident_bf[:])
+        nc.scalar.copy(out=gamma_cols[:], in_=bank[:, : 2 * G // P])
+        if NORM_IN_PSUM:
+            nc.scalar.copy(out=norm_cols[:], in_=bank[:, 32:40])
+            for j in range(8):
+                col = norm_cols[:, j : j + 1].to_broadcast([P, P])
+                nc.tensor.transpose(norm_c[:, j * P : (j + 1) * P], col, ident_bf[:])
+
+        plan = {}
+        passes = {}
+
+        def at(step, rank, fn, *args, vector_passes=0):
+            plan.setdefault(step, []).append((rank, fn, args))
+            passes[step] = passes.get(step, 0) + vector_passes
+
+        VECTOR, SCALAR, SBUF_WORK, LATE, TRANSPOSES = 0, 1, 2, 3, 4
+        for g in range(GROUPS):
+            base = STEPS * g + FIRST
+            if g > 0:
+                at(base - CHAIN, SBUF_WORK, row_rstd, g)
+                at(base - CHAIN, SBUF_WORK, row_terms, g)
+                at(base - CHAIN + 1, LATE, row_pieces, g)
+            at(base - 1, TRANSPOSES, spread_ratio, g)
+            at(base + 1, TRANSPOSES, turn_pieces, g)
+            if g % 2 == 0:
+                at(base, LATE, load_rows, "c_prev", c_prev, g // 2, "c_prev", 2)
+            for s in range(STEPS):
+                at(base + s, SCALAR, scaled_ih, g, s)
+                at(base + s, VECTOR, scaled_hh, g, s, vector_passes=1)
+                at(base + s + SUM_LAG, TRANSPOSES, gate, g, s)
+            for t in range(TILES):
+                done = base + 2 * TILES + SUM_LAG + t * (CELL_GAP if g + 1 < GROUPS else LAST_CELL_GAP)
+                at(done + C0, SBUF_WORK, input_term, g, t)
+                at(done + C1, SBUF_WORK, cell, g, t)
+                at(done + C2, SBUF_WORK, cell_sum, g, t)
+                at(done + C3, SBUF_WORK, cell_stats, g, t, vector_passes=1)
+                at(done + C3 + 1, SBUF_WORK, cell_mean, g, t)
+                at(done + C3 + 1, LATE, cell_rstd, g, t)
+                at(done + C3 + 1, LATE, cell_centred, g, t, vector_passes=1)
+                at(done + C4, SBUF_WORK, cell_bias, g, t, vector_passes=1)
+                at(done + C4 + 1, SBUF_WORK, cell_tanh, g, t)
+                at(done + C5, LATE, hidden, g, t)
+                first = base + CELL_GAP * t
+                at(first, VECTOR, o_centred, g, t, 0, vector_passes=1)
+                at(first, VECTOR, o_centred, g, t, 1, vector_passes=1)
+                at(first + 1, SBUF_WORK, o_sum, g, t, vector_passes=1)
+                at(first + 2, SBUF_WORK, o_bias, g, t, vector_passes=1)
+                at(first + 3, SBUF_WORK, o_gate, g, t)
+        for g in range(2, GROUPS):
+            begin = STEPS * (g - 1) + FIRST - CHAIN - EXTRA
+            at(max(0, begin - 3), SBUF_WORK, open_stats, g)
+            if g % 2 == 0 and g > 2:
+                for m in range(2):
+                    at(begin - 11, SBUF_WORK, load_act, m, g // 2)
+                    at(begin - 8 + 2 * m, TRANSPOSES, turn_act, m, g // 2, 0)
+                    at(begin - 7 + 2 * m, TRANSPOSES, turn_act, m, g // 2, 1)
+                    at(begin - 5 + 2 * m, SBUF_WORK, quantize_act, m, g // 2, vector_passes=1)
+        free = 0
+        for g in range(2, GROUPS):
+            end = STEPS * g + FIRST - CHAIN
+            for i, pair in enumerate(scalar_pairs(g)):
+                first = max(free, end - STEPS - 2 - EXTRA)
+                free = first + 4
+                assert free <= end
+                for c in range(CHUNKS):
+                    at(first + c // 2, SCALAR, scalar_sum, g, pair, c)
+                at(first + 1, LATE, scalar_mean, g, pair)
+                at(first + 2, SBUF_WORK, scalar_squares, g, pair, 0)
+                at(first + 3, SBUF_WORK, scalar_squares, g, pair, 1)
+        todo = [(g, pair, c) for g in range(1, GROUPS) for pair in vector_pairs(g) for c in range(CHUNKS)]
+        todo = todo[HEAD_CHUNKS:]
+        end = STEPS * (GROUPS - 1) + FIRST - CHAIN
+        total = len(todo) + sum(passes.get(s, 0) for s in range(end))
+        spent = 0
+        taken = 0
+        for s in range(end):
+            spent += passes.get(s, 0)
+            while taken < len(todo):
+                g, pair, c = todo[taken]
+                due = STEPS * g + FIRST - CHAIN - 1
+                if (spent >= total * (s + 1) // end and s < due) or s < due - STEPS - 1 - EXTRA:
+                    break
+                taken += 1
+                at(s, VECTOR, vector_stats, g, pair, c)
+                spent += 1
+                if c == CHUNKS - 1:
+                    at(s, LATE, vector_stats_end, g, pair)
+        for step in sorted(plan):
+            for_vector = [e for e in plan[step] if e[0] == VECTOR]
+            for_scalar = [e for e in plan[step] if e[0] == SCALAR]
+            order = []
+            for i in range(max(len(for_vector), len(for_scalar))):
+                order += for_vector[i : i + 1] + for_scalar[i : i + 1]
+            order += sorted((e for e in plan[step] if e[0] > SCALAR), key=lambda e: e[0])
+            for rank, fn, args in order:
+                fn(*args)

@@ -29,23 +29,52 @@ GATE_I, GATE_F, GATE_G, GATE_O = 0, 1, 2, 3
 TURNED_GATES = (GATE_I, GATE_G, GATE_F)
 STEPS = len(TURNED_GATES) * TILES
 PAIRS = 2 * TILES
-SCALAR_PAIRS = (2, 1, 2, 1, 2, 1, 2, 1)
+SCALAR_PAIRS = (0, 2, 2, 1, 2, 1, 2, 1)
+SMALL = 'gpsimd'
+SUMV = 0
+HPOOL = 1
+T1POOL = 1
+T2POOL = 1
+SFIRST = 1
+TURN = 2
 FIRST = 1
-CHAIN = 3
+CHAIN = 4
 UB = 5
-EXTRA = 2
+EXTRA = 0
 VEC_FROM = 7
 HV = 1
 HEAD_CHUNKS = 8
 NORM_IN_PSUM = True
-C0 = 0
+CPER = 3
+PT = 2
+SA = 1
+RA = 2.0
+SB_ = 2
+RB = 2
+SC = 2
+RC = 3
+SD = 3
+SE = 3
+SF = 4
+SH = 5
+OG = 1
+ROG = 2.0
+PSPAN = 4
+OFF = 1
+RV2 = 2.3
+NACT = 0
+RS = 2.07
+RCH = 3
+COFF = 1
+SO = 3
+OJIT = 0
 C1 = 1
 C2 = 2
 C3 = 3
 C4 = 5
 C5 = 6
 VB = 4
-SB = 3
+SB = 4
 SUM_LAG = 2
 CELL_GAP = 3
 LAST_CELL_GAP = 1
@@ -75,20 +104,15 @@ def tile_layernormlstmcell_kernel(
         w_codes = [keep.tile([P, G], U32, name="w_codes%d" % m, align_bytes=64) for m in range(2)]
         w_scales = [keep.tile([P, G], U8, name="w_scales%d" % m, align_bytes=64) for m in range(2)]
         gamma_rows = keep.tile([P, P], BF16, name="gamma_rows")
-        gamma_cols = keep.tile([P, 2 * G // P], F32, name="gamma_cols")
+        gamma_cols = keep.tile([P, 40], F32, name="gamma_cols")
         shift_rhs = keep.tile([P, GATE_O * H], BF16, name="shift_rhs")
         pieces = [keep.tile([P, TILES, P], BF16, name="pieces%d" % i) for i in range(2)]
         gamma_o = [keep.tile([P, H], BF16, name="gamma_o%d" % m) for m in range(2)]
         beta_o_parts = [keep.tile([P, H], BF16, name="beta_o_part%d" % m) for m in range(2)]
         beta_o = keep.tile([P, H], F32, name="beta_o")
-        if NORM_IN_PSUM:
-            norm_c = psum.tile([P, 2 * H], BF16, name="norm_c", bufs=1)
-            norm_cols = keep.tile([P, 8], BF16, name="norm_cols")
-        else:
-            norm_c = keep.tile([P, 2 * H], BF16, name="norm_c")
-        gamma_c_all, beta_c_all = norm_c[:, :H], norm_c[:, H:]
         minus_half = keep.tile([P, PAIRS], F32, name="minus_half")
 
+        minus_one = -1.0
         st = {}
 
         def load_rows(key, src, g, tag, bufs):
@@ -139,8 +163,8 @@ def tile_layernormlstmcell_kernel(
             )
 
         def quantize_act(m, g):
-            codes = work.tile([P, BANK], U32, name="a_codes%d" % m, bufs=3, align_bytes=64)
-            scales = work.tile([P, BANK], U8, name="a_scales%d" % m, bufs=3, align_bytes=64)
+            codes = work.tile([P, BANK], U32, name="a_codes%d" % m, bufs=4, align_bytes=64)
+            scales = work.tile([P, BANK], U8, name="a_scales%d" % m, bufs=4, align_bytes=64)
             nc.vector.quantize_mx(out=codes[:].bitcast(FP8X4), scales=scales[:], in_=st["grouped", m, g][:])
             st["codes", m, g] = (codes, scales)
 
@@ -173,12 +197,12 @@ def tile_layernormlstmcell_kernel(
             )
 
         def open_stats(g):
-            st["mean_var", g] = work.tile([P, PAIRS, 2], F32, name="mean_var", bufs=4)
-            st["squares", g] = work.tile([P, 2, TILES], F32, name="squares", bufs=3)
+            st["mean_var", g] = work.tile([P, PAIRS, 2], F32, name="mean_var", bufs=6)
+            st["squares", g] = work.tile([P, TILES, 2], F32, name="squares", bufs=3)
 
         def vector_stats(g, pair, c):
             if c == 0:
-                st["bn", g, pair] = work.tile([P, CHUNKS, 6], F32, name="bn", bufs=PAIRS)
+                st["bn", g, pair] = work.tile([P, CHUNKS, 6], F32, name="bn", bufs=8)
             bank = vector_bank()
             product_rows(bank, pair // TILES, g, pair % TILES, c)
             nc.vector.bn_stats(out=st["bn", g, pair][:, c, :], in_=bank[:])
@@ -215,43 +239,58 @@ def tile_layernormlstmcell_kernel(
                 func=ACT.Square,
                 scale=-float(G),
                 bias=st["mean_var", g][:, pair, 0:1],
-                accum_out=st["squares", g][:, half, at : at + 1],
+                accum_out=st["squares", g][:, at, half : half + 1],
             )
 
+        def scalar_var(g, pair):
+            halves = st["squares", g][:, pair - TILES, :]
+            nc.scalar.activation(
+                out=halves, in_=halves, func=ACT.Copy, scale=1.0 / G, accum_out=st["mean_var", g][:, pair, 1:2]
+            )
+
+        small = nc.gpsimd if SMALL == "gpsimd" else nc.vector
+
         def row_rstd(g):
-            mean_var, squares = st["mean_var", g], st["squares", g]
-            first = PAIRS - SCALAR_PAIRS[g]
-            var_eps = work.tile([P, PAIRS], F32, name="var_eps", bufs=3)
-            rstd = work.tile([P, PAIRS], F32, name="rstd", bufs=3)
-            minus_mean = work.tile([P, PAIRS], F32, name="minus_mean", bufs=3)
-            low, high = squares[:, 0, first - TILES :], squares[:, 1, first - TILES :]
-            nc.gpsimd.tensor_tensor(low, low, high, ALU.add)
-            nc.gpsimd.tensor_scalar(var_eps[:, :first], mean_var[:, :first, 1], 1.0, EPS, ALU.mult, ALU.add)
-            nc.gpsimd.tensor_scalar(var_eps[:, first:], low, 1.0 / G, EPS, ALU.mult, ALU.add)
+            mean_var = st["mean_var", g]
+            var_eps = work.tile([P, PAIRS], F32, name="var_eps", bufs=5)
+            rstd = work.tile([P, PAIRS], F32, name="rstd", bufs=5)
+            terms = work.tile([P, PAIRS, 4], F32, name="terms", bufs=5)
+            small.tensor_scalar(var_eps[:], mean_var[:, :, 1], 1.0, EPS, ALU.mult, ALU.add)
             nc.gpsimd.tensor_tensor(rstd[:], var_eps[:], minus_half[:], ALU.pow)
-            nc.gpsimd.tensor_scalar(minus_mean[:], mean_var[:, :, 0], -1.0, 0.0, ALU.mult, ALU.add)
-            st["rstd", g], st["var_eps", g], st["minus_mean", g] = rstd, var_eps, minus_mean
+            small.tensor_scalar(terms[:, :, 2], mean_var[:, :, 0], -1.0, 0.0, ALU.mult, ALU.add)
+            st["rstd", g], st["var_eps", g], st["terms", g] = rstd, var_eps, terms
 
-        def row_terms(g):
-            rstd, var_eps, minus_mean = st["rstd", g], st["var_eps", g], st["minus_mean", g]
-            terms = work.tile([P, TILES, 4], F32, name="terms", bufs=3)
-            ratio = work.tile([P, TILES], F32, name="ratio", bufs=3)
-            nc.gpsimd.tensor_tensor(terms[:, :, 0], var_eps[:, :TILES], rstd[:, :TILES], ALU.mult)
-            nc.gpsimd.tensor_tensor(terms[:, :, 1], var_eps[:, :TILES], rstd[:, :TILES], ALU.mult)
-            nc.gpsimd.tensor_tensor(ratio[:], terms[:, :, 0], rstd[:, TILES:], ALU.mult)
-            nc.gpsimd.tensor_copy(out=terms[:, :, 2], in_=minus_mean[:, :TILES])
-            nc.gpsimd.tensor_tensor(terms[:, :, 3], minus_mean[:, TILES:], ratio[:], ALU.mult)
-            st["terms", g], st["ratio", g] = terms, ratio
+        def row_std(g):
+            rstd, var_eps, terms = st["rstd", g], st["var_eps", g], st["terms", g]
+            twice = [P, TILES, 2]
+            small.tensor_tensor(
+                terms[:, :TILES, 0:2],
+                var_eps[:, :TILES].unsqueeze(2).to_broadcast(twice),
+                rstd[:, :TILES].unsqueeze(2).to_broadcast(twice),
+                ALU.mult,
+            )
 
-        def row_pieces(g):
+        def row_ratio(g):
+            ratio = work.tile([P, TILES], F32, name="ratio", bufs=5)
+            small.tensor_tensor(ratio[:], st["terms", g][:, :TILES, 0], st["rstd", g][:, TILES:], ALU.mult)
+            st["ratio", g] = ratio
+
+        def row_shift(g):
             terms = st["terms", g]
-            rest = work.tile([P, TILES, 4], F32, name="rest", bufs=3)
+            small.tensor_tensor(terms[:, :TILES, 3], terms[:, TILES:, 2], st["ratio", g][:], ALU.mult)
+
+        def row_piece(g, i):
             split = pieces[g % 2][:, :, 0:12].rearrange("p t (v s) -> p t v s", s=3)
-            nc.gpsimd.tensor_copy(out=split[:, :, :, 0], in_=terms[:])
-            nc.gpsimd.tensor_tensor(rest[:], terms[:], split[:, :, :, 0], ALU.subtract)
-            nc.gpsimd.tensor_copy(out=split[:, :, :, 1], in_=rest[:])
-            nc.gpsimd.tensor_tensor(rest[:], rest[:], split[:, :, :, 1], ALU.subtract)
-            nc.gpsimd.tensor_copy(out=split[:, :, :, 2], in_=rest[:])
+            small.tensor_copy(out=split[:, :, :, i], in_=st["rest", g] if i else st["terms", g][:, :TILES, :])
+
+        def row_rest(g, i):
+            split = pieces[g % 2][:, :, 0:12].rearrange("p t (v s) -> p t v s", s=3)
+            rest = work.tile([P, TILES, 4], F32, name="rest", bufs=4)
+            before = st["rest", g] if i else st["terms", g][:, :TILES, :]
+            small.tensor_tensor(rest[:], before, split[:, :, :, i], ALU.subtract)
+            st["rest", g] = rest[:]
+
+        chain = [(row_std,), (row_ratio,), (row_shift,), (row_piece, 0), (row_rest, 0), (row_piece, 1), (row_rest, 1), (row_piece, 2)]
 
         def spread_ratio(g):
             bank = scalar_bank()
@@ -329,7 +368,7 @@ def tile_layernormlstmcell_kernel(
         def o_centred(g, t, m):
             bank = vector_bank()
             product_rows(bank, m, g, t, GATE_O)
-            u = work.tile([P, H], F32, name="o_part%d" % m, bufs=2 + 2 * m)
+            u = work.tile([P, H], F32, name="o_part%d" % m, bufs=3)
             mean = st["mean_var", g][:, m * TILES + t, 0:1]
             nc.vector.scalar_tensor_tensor(u[:], bank[:], mean, gamma_o[m][:], ALU.subtract, ALU.mult)
             st["o_part", m, g, t] = u
@@ -352,13 +391,13 @@ def tile_layernormlstmcell_kernel(
 
         def input_term(g, t):
             i_gate = st["gate", GATE_I, g, t]
-            nc.gpsimd.tensor_tensor(i_gate[:], i_gate[:], st["gate", GATE_G, g, t][:], ALU.mult)
+            (nc.gpsimd if T1POOL and g < VEC_FROM + 1 else nc.vector).tensor_tensor(i_gate[:], i_gate[:], st["gate", GATE_G, g, t][:], ALU.mult)
             st["input_term", g, t] = i_gate
 
         def cell(g, t):
             f_gate = st["gate", GATE_F, g, t]
-            c_new = work.tile([P, H], F32, name="c_new", bufs=3)
-            engine = nc.vector if g >= VEC_FROM else nc.gpsimd
+            c_new = work.tile([P, H], F32, name="c_new", bufs=4)
+            engine = nc.vector if g >= VEC_FROM or not T2POOL else nc.gpsimd
             engine.tensor_tensor(f_gate[:], f_gate[:], st["c_prev", g // 2][:, g % 2 * TILES + t, :], ALU.mult)
             st["c", g, t] = c_new
 
@@ -366,16 +405,31 @@ def tile_layernormlstmcell_kernel(
             f_gate = st["gate", GATE_F, g, t]
             c_new = st["c", g, t]
             engine = nc.vector if g >= VEC_FROM else nc.gpsimd
-            engine.tensor_tensor(c_new[:], f_gate[:], st["input_term", g, t][:], ALU.add)
+            if SUMV:
+                total = work.tile([P, 4], F32, name="c_total", bufs=3)
+                nc.vector.scalar_tensor_tensor(c_new[:], f_gate[:], 1.0, st["input_term", g, t][:], ALU.mult, ALU.add, accum_out=total[:, 0:1])
+                st["c_total", g, t] = total
+            else:
+                engine.tensor_tensor(c_new[:], f_gate[:], st["input_term", g, t][:], ALU.add)
             row = (g * TILES + t) * P
             nc.sync.dma_start(out=out_1[row : row + P, :], in_=c_new[:])
 
         def cell_stats(g, t):
+            if SUMV:
+                mean_var = work.tile([P, 2], F32, name="c_mean_var", bufs=3)
+                st["c_mean", g, t] = mean_var
+                nc.scalar.activation(out=mean_var[:, 0:1], in_=st["c_total", g, t][:, 0:1], func=ACT.Copy, scale=1.0 / H)
+                return
             bn = work.tile([P, 6], F32, name="c_bn")
             nc.vector.bn_stats(out=bn[:], in_=st["c", g, t][:])
             st["c_bn", g, t] = bn
 
         def cell_mean(g, t):
+            if SUMV:
+                mean_var = st["c_mean", g, t]
+                junk = work.tile([P, H], F32, name="c_squares")
+                nc.scalar.activation(out=junk[:], in_=st["c", g, t][:], func=ACT.Square, scale=-1.0, bias=mean_var[:, 0:1], accum_out=mean_var[:, 1:2])
+                return
             mean_var = work.tile([P, 2], F32, name="c_mean_var", bufs=3)
             nc.vector.bn_aggr(out=mean_var[:], in_=st["c_bn", g, t][:])
             st["c_mean", g, t] = mean_var
@@ -384,29 +438,46 @@ def tile_layernormlstmcell_kernel(
             mean_var = st["c_mean", g, t]
             var_eps = work.tile([P, 1], F32, name="c_var_eps", bufs=3)
             rstd = work.tile([P, 1], F32, name="c_rstd", bufs=3)
-            nc.gpsimd.tensor_scalar(var_eps[:], mean_var[:, 1:2], 1.0, EPS, ALU.mult, ALU.add)
+            small.tensor_scalar(var_eps[:], mean_var[:, 1:2], 1.0 / H if SUMV else 1.0, EPS, ALU.mult, ALU.add)
             nc.gpsimd.tensor_tensor(rstd[:], var_eps[:], minus_half[:, 0:1], ALU.pow)
             st["c_rstd", g, t] = rstd
+            if NACT:
+                shift = work.tile([P, 1], F32, name="c_shift", bufs=3)
+                small.tensor_scalar(shift[:], mean_var[:, 0:1], rstd[:], minus_one, ALU.mult, ALU.mult)
+                st["c_shift", g, t] = shift
 
-        def cell_centred(g, t):
-            y = work.tile([P, H], F32, name="c_norm", bufs=4)
+        def cell_normed(g, t):
+            y = work.tile([P, H], F32, name="c_norm", bufs=3)
             mean = st["c_mean", g, t][:, 0:1]
-            nc.vector.scalar_tensor_tensor(y[:], st["c", g, t][:], mean, gamma_c_all, ALU.subtract, ALU.mult)
+            if NACT:
+                nc.scalar.activation(out=y[:], in_=st["c", g, t][:], func=ACT.Identity, scale=st["c_rstd", g, t][:], bias=st["c_shift", g, t][:])
+            else:
+                nc.vector.tensor_scalar(y[:], st["c", g, t][:], mean, st["c_rstd", g, t][:], ALU.subtract, ALU.mult)
             st["c_norm", g, t] = y
-
-        def cell_bias(g, t):
-            y = st["c_norm", g, t]
-            nc.vector.scalar_tensor_tensor(y[:], y[:], st["c_rstd", g, t][:], beta_c_all, ALU.mult, ALU.add)
 
         def cell_tanh(g, t):
             y = st["c_norm", g, t]
-            nc.scalar.activation(out=y[:], in_=y[:], func=ACT.Tanh)
+            bank = scalar_bank()
+            for i in range(4):
+                nc.tensor.transpose(bank[:, i * P : (i + 1) * P], y[:, i * P : (i + 1) * P], ident[:])
+            z = work.tile([P, H], F32, name="c_tanh", bufs=3)
+            for i in range(4):
+                nc.scalar.activation(
+                    out=z[:, i * P : (i + 1) * P],
+                    in_=bank[:, i * P : (i + 1) * P],
+                    func=ACT.Tanh,
+                    scale=gamma_cols[:, 32 + i : 33 + i],
+                    bias=gamma_cols[:, 36 + i : 37 + i],
+                )
+            st["c_tanh", g, t] = z
 
         def hidden(g, t):
-            y = st["c_norm", g, t]
-            h_new = work.tile([P, H], F32, name="h_new")
-            engine = nc.vector if g == GROUPS - 1 and t % 2 == 1 else nc.gpsimd
-            engine.tensor_tensor(h_new[:], y[:], st["gate", GATE_O, g, t][:], ALU.mult)
+            z = st["c_tanh", g, t]
+            bank = vector_bank()
+            for i in range(4):
+                nc.tensor.transpose(bank[:, i * P : (i + 1) * P], z[:, i * P : (i + 1) * P], ident[:])
+            h_new = work.tile([P, H], F32, name="h_new", bufs=3)
+            nc.vector.tensor_tensor(h_new[:], bank[:], st["gate", GATE_O, g, t][:], ALU.mult)
             row = (g * TILES + t) * P
             nc.sync.dma_start(out=out_0[row : row + P, :], in_=h_new[:])
 
@@ -419,12 +490,12 @@ def tile_layernormlstmcell_kernel(
         def scalar_pairs(g):
             return list(range(PAIRS - SCALAR_PAIRS[g], PAIRS))
 
-        load_act(0, 0)
         load_weight(0, 0)
+        load_act(0, 0)
         load_weight(0, 1)
         load_weight(0, 2)
-        load_weight(0, 3)
         load_act(1, 0)
+        load_weight(0, 3)
         make_identity(nc, ident[:])
         make_identity(nc, ident_bf[:])
         nc.gpsimd.memset(gamma_rows[:], 0.0)
@@ -433,90 +504,82 @@ def tile_layernormlstmcell_kernel(
         for i in range(2):
             nc.gpsimd.memset(pieces[i][:], 0.0)
         open_stats(0)
+        open_stats(1)
+        ih_tiles = [(g, t) for g in range(2) for t in range(TILES)]
+
+        def head_stats(c, first, last):
+            for g, t in ih_tiles[first:last]:
+                vector_stats(g, t, c)
+
+        interleave_weight(0, 0, nc.vector.tensor_copy)
+        load_weight(1, 0)
         turn_act(0, 0, 0)
         turn_act(0, 0, 1)
-        load_weight(1, 0)
-        interleave_weight(0, 0, nc.vector.tensor_copy)
         load_weight(1, 1)
-        quantize_act(0, 0)
-        interleave_weight(0, 1, nc.scalar.copy)
         quantize_weight(0, 0)
+        interleave_weight(0, 1, nc.scalar.copy)
         load_weight(1, 2)
+        quantize_act(0, 0)
         interleave_weight(0, 2, nc.vector.tensor_copy)
         load_weight(1, 3)
-        quantize_weight(0, 1)
-        interleave_weight(0, 3, nc.vector.tensor_copy)
-        load_act(0, 1)
+        head_stats(0, 0, 1)
         quantize_weight(0, 2)
+        quantize_weight(0, 1)
         turn_act(1, 0, 0)
         turn_act(1, 0, 1)
-        load_act(1, 1)
-        vector_stats(0, 0, 0)
-        quantize_weight(0, 3)
-        interleave_weight(1, 0, nc.scalar.copy)
-        vector_stats(0, 0, 1)
+        load_act(0, 1)
+        head_stats(0, 1, 3)
         quantize_act(1, 0)
-        interleave_weight(1, 1, nc.vector.tensor_copy)
-        vector_stats(0, 0, 2)
+        interleave_weight(0, 3, nc.scalar.copy)
+        load_act(1, 1)
+        interleave_weight(1, 0, nc.vector.tensor_copy)
+        head_stats(0, 3, 4)
         quantize_weight(1, 0)
-        interleave_weight(1, 2, nc.scalar.copy)
-        vector_stats(0, 0, 3)
-        quantize_weight(1, 1)
-        interleave_weight(1, 3, nc.vector.tensor_copy)
-        vector_stats(0, 1, 0)
+        quantize_weight(0, 3)
+        interleave_weight(1, 1, nc.scalar.copy)
+        interleave_weight(1, 2, nc.vector.tensor_copy)
+        head_stats(1, 0, 1)
         quantize_weight(1, 2)
-        vector_stats(0, 1, 1)
+        quantize_weight(1, 1)
+        interleave_weight(1, 3, nc.scalar.copy)
+        head_stats(1, 1, 2)
+        head_stats(2, 0, 2)
         quantize_weight(1, 3)
         for m, gamma in enumerate((gamma_ih, gamma_hh)):
             nc.sync.dma_start(
                 out=gamma_rows[m * G // P : (m + 1) * G // P, :], in_=gamma.rearrange("(j n) -> j n", n=P)
             )
-        if NORM_IN_PSUM:
+        if True:
             for m, vec in enumerate((gamma_c, beta_c)):
                 nc.sync.dma_start(out=gamma_rows[32 + 4 * m : 36 + 4 * m, :], in_=vec.rearrange("(j n) -> j n", n=P))
         for v, vec in enumerate((beta_ih, beta_hh, gamma_ih, gamma_hh)):
             nc.sync.dma_start(out=shift_rhs[3 * v : 3 * v + 3, :], in_=vec[: GATE_O * H].partition_broadcast(3))
         for dst, vec in zip(gamma_o + beta_o_parts, (gamma_ih, gamma_hh, beta_ih, beta_hh)):
             nc.sync.dma_start(out=dst[:], in_=vec[GATE_O * H :].partition_broadcast(P))
-        if not NORM_IN_PSUM:
-            nc.sync.dma_start(out=gamma_c_all, in_=gamma_c.partition_broadcast(P))
-            nc.sync.dma_start(out=beta_c_all, in_=beta_c.partition_broadcast(P))
-
-        vector_list = [(0, pair, c) for pair in vector_pairs(0) for c in range(CHUNKS)][6:]
-        vector_list += [(1, pair, c) for pair in vector_pairs(1) for c in range(CHUNKS)][:HEAD_CHUNKS]
+        vector_list = [(vector_stats, 0, t, 3) for t in range(TILES)]
+        vector_list += [(vector_stats, 0, TILES + t, c) for t in range(TILES) for c in range(CHUNKS)]
+        vector_list += [(vector_stats_end, 0, pair) for pair in range(PAIRS)] + [(row_rstd, 0)]
+        rest_of_ih = [(vector_stats, 1, t, c) for t in range(TILES) for c in range(1, CHUNKS)]
+        for n, entry in enumerate(chain):
+            vector_list += rest_of_ih[n : n + 1] + [(entry[0], 0) + entry[1:]]
+        vector_list += [(vector_stats_end, 1, t) for t in range(TILES)]
         scalar_list = []
-        for g, pair in [(0, pair) for pair in scalar_pairs(0)] + [(1, scalar_pairs(1)[0])]:
-            scalar_list += [(scalar_sum, g, pair, c) for c in range(CHUNKS)]
-            scalar_list += [(scalar_mean, g, pair)]
-            scalar_list += [(scalar_squares, g, pair, 0), (scalar_squares, g, pair, 1)]
-            if g == 0 and pair == scalar_pairs(0)[-1]:
-                scalar_list += [(row_rstd, 0), (row_terms, 0), (row_pieces, 0)]
-        open_stats(1)
-        vector_stats_end(0, 0)
+        for pair in scalar_pairs(1):
+            m = pair - TILES
+            scalar_list += [(scalar_sum, 1, pair, c) for c in range(CHUNKS)]
+            scalar_list += [(scalar_mean, 1, pair)]
+            scalar_list += [(turn_act, m, 1, 0), (turn_act, m, 1, 1), (quantize_act, m, 1)]
+            scalar_list += [(scalar_squares, 1, pair, 0), (scalar_squares, 1, pair, 1), (scalar_var, 1, pair)]
         nc.gpsimd.tensor_tensor(beta_o[:], beta_o_parts[0][:], beta_o_parts[1][:], ALU.add)
         taken = 0
         for n, entry in enumerate(scalar_list):
             entry[0](*entry[1:])
             while taken < len(vector_list) * (n + 1) // len(scalar_list):
-                g, pair, c = vector_list[taken]
+                vector_list[taken][0](*vector_list[taken][1:])
                 taken += 1
-                vector_stats(g, pair, c)
-                if c == 0 and taken > 2:
-                    vector_stats_end(*vector_list[taken - 2][:2])
-        if HEAD_CHUNKS % CHUNKS == 0:
-            vector_stats_end(*vector_list[-1][:2])
-        for m in range(2):
-            turn_act(m, 1, 0)
-            turn_act(m, 1, 1)
-            quantize_act(m, 1)
         bank = scalar_bank(BF16)
         nc.tensor.transpose(bank[:, :P], gamma_rows[:], ident_bf[:])
-        nc.scalar.copy(out=gamma_cols[:], in_=bank[:, : 2 * G // P])
-        if NORM_IN_PSUM:
-            nc.scalar.copy(out=norm_cols[:], in_=bank[:, 32:40])
-            for j in range(8):
-                col = norm_cols[:, j : j + 1].to_broadcast([P, P])
-                nc.tensor.transpose(norm_c[:, j * P : (j + 1) * P], col, ident_bf[:])
+        nc.scalar.copy(out=gamma_cols[:], in_=bank[:, :40])
 
         plan = {}
         passes = {}
@@ -529,11 +592,11 @@ def tile_layernormlstmcell_kernel(
         for g in range(GROUPS):
             base = STEPS * g + FIRST
             if g > 0:
-                at(base - CHAIN, SBUF_WORK, row_rstd, g)
-                at(base - CHAIN, SBUF_WORK, row_terms, g)
-                at(base - CHAIN + 1, LATE, row_pieces, g)
+                at(base - CHAIN, LATE, row_rstd, g)
+                for n, entry in enumerate(chain):
+                    at(base - CHAIN + COFF + n // CPER, RCH, entry[0], g, *entry[1:])
             at(base - 1, TRANSPOSES, spread_ratio, g)
-            at(base + 1, TRANSPOSES, turn_pieces, g)
+            at(base + PT - 1, TRANSPOSES, turn_pieces, g)
             if g % 2 == 0:
                 at(base, LATE, load_rows, "c_prev", c_prev, g // 2, "c_prev", 2)
             for s in range(STEPS):
@@ -542,45 +605,45 @@ def tile_layernormlstmcell_kernel(
                 at(base + s + SUM_LAG, TRANSPOSES, gate, g, s)
             for t in range(TILES):
                 done = base + 2 * TILES + SUM_LAG + t * (CELL_GAP if g + 1 < GROUPS else LAST_CELL_GAP)
-                at(done + C0, SBUF_WORK, input_term, g, t)
-                at(done + C1, SBUF_WORK, cell, g, t)
-                at(done + C2, SBUF_WORK, cell_sum, g, t)
-                at(done + C3, SBUF_WORK, cell_stats, g, t, vector_passes=1)
-                at(done + C3 + 1, SBUF_WORK, cell_mean, g, t)
-                at(done + C3 + 1, LATE, cell_rstd, g, t)
-                at(done + C3 + 1, LATE, cell_centred, g, t, vector_passes=1)
-                at(done + C4, SBUF_WORK, cell_bias, g, t, vector_passes=1)
-                at(done + C4 + 1, SBUF_WORK, cell_tanh, g, t)
-                at(done + C5, LATE, hidden, g, t)
-                first = base + CELL_GAP * t
-                at(first, VECTOR, o_centred, g, t, 0, vector_passes=1)
-                at(first, VECTOR, o_centred, g, t, 1, vector_passes=1)
-                at(first + 1, SBUF_WORK, o_sum, g, t, vector_passes=1)
-                at(first + 2, SBUF_WORK, o_bias, g, t, vector_passes=1)
-                at(first + 3, SBUF_WORK, o_gate, g, t)
+                at(done + C1, 2.05, input_term, g, t, vector_passes=1 - T1POOL)
+                at(done + C1, 2.06, cell, g, t, vector_passes=1 - T2POOL)
+                at(done + C2, RS, cell_sum, g, t, vector_passes=SUMV)
+                at(done + C2 + SA, RA, cell_stats, g, t, vector_passes=1 - SUMV)
+                at(done + C2 + SB_, RB, cell_mean, g, t)
+                at(done + C2 + SC, RC, cell_rstd, g, t)
+                at(done + C2 + SD, 2.2, cell_normed, g, t, vector_passes=0.5 - 0.5 * NACT)
+                at(done + C2 + SF, 4.1, cell_tanh, g, t)
+                at(done + C2 + SH, 4.2, hidden, g, t, vector_passes=1)
+                first = done + C2 + SO if g < OJIT else base + CELL_GAP * t + OFF
+                at(first - 1, VECTOR, o_centred, g, t, 0, vector_passes=1)
+                at(first - 1, VECTOR, o_centred, g, t, 1, vector_passes=1)
+                at(first, 2.1, o_sum, g, t, vector_passes=1)
+                at(first, RV2, o_bias, g, t, vector_passes=1)
+                at(first + OG, ROG, o_gate, g, t)
+        ready = {1: 0}
+        for j in range(2, GROUPS // 2):
+            begin = TURN + (2 * STEPS + 1) * (j - 2)
+            for m in range(2):
+                at(begin - 4, SBUF_WORK, load_act, m, j)
+                at(begin + 2 * m, TRANSPOSES, turn_act, m, j, 0)
+                at(begin + 1 + 2 * m, TRANSPOSES, turn_act, m, j, 1)
+                at(begin + 3 + 2 * m, SBUF_WORK, quantize_act, m, j, vector_passes=1)
+            ready[j] = begin + 6
+        opened = {}
+        first = SFIRST
         for g in range(2, GROUPS):
-            begin = STEPS * (g - 1) + FIRST - CHAIN - EXTRA
-            at(max(0, begin - 3), SBUF_WORK, open_stats, g)
-            if g % 2 == 0 and g > 2:
-                for m in range(2):
-                    at(begin - 11, SBUF_WORK, load_act, m, g // 2)
-                    at(begin - 8 + 2 * m, TRANSPOSES, turn_act, m, g // 2, 0)
-                    at(begin - 7 + 2 * m, TRANSPOSES, turn_act, m, g // 2, 1)
-                    at(begin - 5 + 2 * m, SBUF_WORK, quantize_act, m, g // 2, vector_passes=1)
-        free = 0
-        for g in range(2, GROUPS):
-            end = STEPS * g + FIRST - CHAIN
-            for i, pair in enumerate(scalar_pairs(g)):
-                first = max(free, end - STEPS - 2 - EXTRA)
-                free = first + 4
-                assert free <= end
+            for pair in scalar_pairs(g):
+                opened.setdefault(g, first)
+                assert first >= ready[g // 2]
                 for c in range(CHUNKS):
                     at(first + c // 2, SCALAR, scalar_sum, g, pair, c)
                 at(first + 1, LATE, scalar_mean, g, pair)
                 at(first + 2, SBUF_WORK, scalar_squares, g, pair, 0)
-                at(first + 3, SBUF_WORK, scalar_squares, g, pair, 1)
-        todo = [(g, pair, c) for g in range(1, GROUPS) for pair in vector_pairs(g) for c in range(CHUNKS)]
-        todo = todo[HEAD_CHUNKS:]
+                at(first + PSPAN - 1, 2.5, scalar_squares, g, pair, 1)
+                at(first + PSPAN, 2.0, scalar_var, g, pair)
+                first += PSPAN
+            assert first <= STEPS * g + FIRST - CHAIN, (g, first)
+        todo = [(g, pair, c) for g in range(2, GROUPS) for pair in vector_pairs(g) for c in range(CHUNKS)]
         end = STEPS * (GROUPS - 1) + FIRST - CHAIN
         total = len(todo) + sum(passes.get(s, 0) for s in range(end))
         spent = 0
@@ -590,13 +653,16 @@ def tile_layernormlstmcell_kernel(
             while taken < len(todo):
                 g, pair, c = todo[taken]
                 due = STEPS * g + FIRST - CHAIN - 1
-                if (spent >= total * (s + 1) // end and s < due) or s < due - STEPS - 1 - EXTRA:
+                if (spent >= total * (s + 1) // end and s < due) or s < ready[g // 2]:
                     break
                 taken += 1
+                opened[g] = min(opened.get(g, s), s)
                 at(s, VECTOR, vector_stats, g, pair, c)
                 spent += 1
                 if c == CHUNKS - 1:
                     at(s, LATE, vector_stats_end, g, pair)
+        for g in range(2, GROUPS):
+            at(opened[g] - 1, SBUF_WORK, open_stats, g)
         for step in sorted(plan):
             for_vector = [e for e in plan[step] if e[0] == VECTOR]
             for_scalar = [e for e in plan[step] if e[0] == SCALAR]

@@ -19,72 +19,35 @@ ACT = mybir.ActivationFunctionType
 P = 128
 PACK = 4
 BANK = 512
-TILES = 2
-LOAD_TILES = 4
-ROWS = TILES * P
-PER_BANK = BANK // ROWS
-GROUPS = B // (P * TILES)
 CHUNKS = G // BANK
+BLOCKS = H // P
+IH, HH = 0, 1
 GATE_I, GATE_F, GATE_G, GATE_O = 0, 1, 2, 3
-TURNED_GATES = (GATE_I, GATE_G, GATE_F)
-STEPS = len(TURNED_GATES) * TILES
+GATE_ORDER = (GATE_I, GATE_G, GATE_F, GATE_O)
+
+LOAD_TILES = 4
+TILES = 2
+ROWS = TILES * P
+GROUPS = B // ROWS
+LAST = GROUPS - 1
+PER_LOAD = LOAD_TILES // TILES
+PER_BANK = BANK // ROWS
 PAIRS = 2 * TILES
-SCALAR_PAIRS = (0, 2, 2, 1, 2, 1, 2, 1)
-SMALL = 'gpsimd'
-SUMV = 0
-HPOOL = 1
-T1POOL = 1
-T2POOL = 1
-SFIRST = 1
-TURN = 2
-FIRST = 1
-CHAIN = 4
-UB = 5
-EXTRA = 0
-VEC_FROM = 7
-HV = 1
-HEAD_CHUNKS = 8
-NORM_IN_PSUM = True
-CPER = 3
-PT = 2
-SA = 1
-RA = 2.0
-SB_ = 2
-RB = 2
-SC = 2
-RC = 3
-SD = 3
-SE = 3
-SF = 4
-SH = 5
-OG = 1
-ROG = 2.0
-PSPAN = 4
-OFF = 1
-RV2 = 2.3
-NACT = 0
-RS = 2.07
-RCH = 3
-COFF = 1
-SO = 3
-OJIT = 0
-C1 = 1
-C2 = 2
-C3 = 3
-C4 = 5
-C5 = 6
-VB = 4
-SB = 4
-SUM_LAG = 2
-CELL_GAP = 3
-LAST_CELL_GAP = 1
+TERMS, PIECES = 4, 3
+NORM_COL = 2 * G // P
+
+PERIOD = 3 * TILES
+TILE_GAP = PERIOD // TILES
+FIRST = 3
+FACTOR_LEAD = 4
+SCALAR_SPAN = 4
 
 
 def tile_layernormlstmcell_kernel(
     tc, x, h_prev, c_prev, W_ih, W_hh, gamma_ih, beta_ih, gamma_hh, beta_hh, gamma_c, beta_c, out_0, out_1
 ):
     nc = tc.nc
-    acts = (x, h_prev)
+    row_inputs = (x, h_prev)
     weights = (W_ih, W_hh)
 
     with ExitStack() as ctx:
@@ -94,86 +57,88 @@ def tile_layernormlstmcell_kernel(
         ctx.enter_context(tc.manual_schedule())
 
         def vector_bank():
-            return psum.tile([P, BANK], F32, name="vector_bank", tag="vector_bank", bufs=VB)
+            return psum.tile([P, BANK], F32, name="vector_bank", tag="vector_bank")
 
         def scalar_bank(dtype=F32):
-            return psum.tile([P, BANK], dtype, name="scalar_bank", tag="scalar_bank", bufs=SB)
+            return psum.tile([P, BANK], dtype, name="scalar_bank", tag="scalar_bank")
 
         ident = keep.tile([P, P], F32, name="ident")
         ident_bf = keep.tile([P, P], BF16, name="ident_bf")
-        w_codes = [keep.tile([P, G], U32, name="w_codes%d" % m, align_bytes=64) for m in range(2)]
-        w_scales = [keep.tile([P, G], U8, name="w_scales%d" % m, align_bytes=64) for m in range(2)]
-        gamma_rows = keep.tile([P, P], BF16, name="gamma_rows")
-        gamma_cols = keep.tile([P, 40], F32, name="gamma_cols")
-        shift_rhs = keep.tile([P, GATE_O * H], BF16, name="shift_rhs")
+        w_codes = [keep.tile([P, G], U32, name="w_codes%d" % m, align_bytes=64) for m in (IH, HH)]
+        w_scales = [keep.tile([P, G], U8, name="w_scales%d" % m, align_bytes=64) for m in (IH, HH)]
+        gain_rows = keep.tile([P, P], BF16, name="gain_rows")
+        gain_cols = keep.tile([P, NORM_COL + 2 * BLOCKS], F32, name="gain_cols")
+        shift_rhs = keep.tile([P, G], BF16, name="shift_rhs")
         pieces = [keep.tile([P, TILES, P], BF16, name="pieces%d" % i) for i in range(2)]
-        gamma_o = [keep.tile([P, H], BF16, name="gamma_o%d" % m) for m in range(2)]
-        beta_o_parts = [keep.tile([P, H], BF16, name="beta_o_part%d" % m) for m in range(2)]
+        gamma_o = [keep.tile([P, H], BF16, name="gamma_o%d" % m) for m in (IH, HH)]
+        beta_o_parts = [keep.tile([P, H], BF16, name="beta_o_part%d" % m) for m in (IH, HH)]
         beta_o = keep.tile([P, H], F32, name="beta_o")
         minus_half = keep.tile([P, PAIRS], F32, name="minus_half")
 
-        minus_one = -1.0
-        st = {}
+        held = {}
 
-        def load_rows(key, src, g, tag, bufs):
+        def load_rows(src, load, tag, bufs):
             raw = work.tile([P, LOAD_TILES, K], BF16, name=tag, tag=tag, bufs=bufs)
-            rows = src[g * LOAD_TILES * P : (g + 1) * LOAD_TILES * P, :]
+            rows = src[load * LOAD_TILES * P : (load + 1) * LOAD_TILES * P, :]
             nc.sync.dma_start(out=raw[:], in_=rows.rearrange("(t p) k -> p t k", p=P))
-            st[key, g] = raw
+            return raw
 
-        def load_act(m, g):
-            load_rows(("raw", m), acts[m], g, "raw", 6)
+        def load_input(m, load):
+            held["raw", m, load] = load_rows(row_inputs[m], load, "raw", 6)
+
+        def load_cell(load):
+            held["c_prev", load] = load_rows(c_prev, load, "c_prev", 2)
 
         def load_weight(m, c):
             raw = work.tile([P, PACK, BANK], BF16, name="raw", tag="raw", bufs=6)
             cols = weights[m][:, c * BANK : (c + 1) * BANK]
             nc.sync.dma_start(out=raw[:], in_=cols.rearrange("(p j) n -> p j n", j=PACK))
-            st["w_raw", m, c] = raw
+            held["w_raw", m, c] = raw
 
         def grouped_tile():
-            return work.tile([P, BANK * PACK], BF16, name="grouped", tag="grouped", bufs=3, align_bytes=64)
+            return work.tile([P, BANK * PACK], BF16, name="grouped", tag="grouped", bufs=4, align_bytes=64)
 
         def interleave_weight(m, c, copy):
             grouped = grouped_tile()
             copy(
-                out=grouped[:].rearrange("p (c i j) -> p c j i", i=4, j=PACK),
-                in_=st["w_raw", m, c][:].rearrange("p j (c i) -> p c j i", i=4),
+                out=grouped[:].rearrange("p (n i j) -> p n j i", i=4, j=PACK),
+                in_=held["w_raw", m, c][:].rearrange("p j (n i) -> p n j i", i=4),
             )
-            st["w_grouped", m, c] = grouped
+            held["w_grouped", m, c] = grouped
 
         def quantize_weight(m, c):
             cols = slice(c * BANK, (c + 1) * BANK)
             nc.vector.quantize_mx(
-                out=w_codes[m][:, cols].bitcast(FP8X4), scales=w_scales[m][:, cols], in_=st["w_grouped", m, c][:]
+                out=w_codes[m][:, cols].bitcast(FP8X4), scales=w_scales[m][:, cols], in_=held["w_grouped", m, c][:]
             )
 
-        def turn_act(m, g, half):
+        def turn_input(m, load, half):
             if half == 0:
-                st["grouped", m, g] = grouped_tile()
+                held["grouped", m, load] = grouped_tile()
             bank = scalar_bank()
             for i in range(2):
-                words = st[("raw", m), g][:, 2 * half + i, :].bitcast(F32)
+                words = held["raw", m, load][:, 2 * half + i, :].bitcast(F32)
                 for u in range(2):
-                    at = (2 * i + u) * P
-                    nc.tensor.transpose(bank[:, at : at + P], words[:, u : K // 2 : 2], ident[:])
-            dst = st["grouped", m, g][:].bitcast(F32)[:, half * BANK : (half + 1) * BANK]
+                    col = (2 * i + u) * P
+                    nc.tensor.transpose(bank[:, col : col + P], words[:, u : K // 2 : 2], ident[:])
+            dst = held["grouped", m, load][:].bitcast(F32)[:, half * BANK : (half + 1) * BANK]
             nc.scalar.copy(
                 out=dst.rearrange("p (i r u) -> p i r u", i=2, u=2),
                 in_=bank[:].rearrange("p (i u r) -> p i r u", i=2, u=2),
             )
 
-        def quantize_act(m, g):
-            codes = work.tile([P, BANK], U32, name="a_codes%d" % m, bufs=4, align_bytes=64)
-            scales = work.tile([P, BANK], U8, name="a_scales%d" % m, bufs=4, align_bytes=64)
-            nc.vector.quantize_mx(out=codes[:].bitcast(FP8X4), scales=scales[:], in_=st["grouped", m, g][:])
-            st["codes", m, g] = (codes, scales)
+        def quantize_input(m, load):
+            codes = work.tile([P, BANK], U32, name="row_codes%d" % m, bufs=4, align_bytes=64)
+            scales = work.tile([P, BANK], U8, name="row_scales%d" % m, bufs=4, align_bytes=64)
+            nc.vector.quantize_mx(out=codes[:].bitcast(FP8X4), scales=scales[:], in_=held["grouped", m, load][:])
+            held["codes", m, load] = (codes, scales)
 
         def product_rows(bank, m, g, t, c):
-            codes, scales = st["codes", m, g // 2]
-            t += g % 2 * TILES
-            rows, cols = slice(t * P, (t + 1) * P), slice(c * BANK, (c + 1) * BANK)
+            codes, scales = held["codes", m, g // PER_LOAD]
+            first = g % PER_LOAD * ROWS + t * P
+            rows, cols = slice(first, first + P), slice(c * BANK, (c + 1) * BANK)
             nc.tensor.matmul_mx(
-                out=bank[:],
+                out=bank,
                 lhsT=codes[:, rows].bitcast(FP8X4),
                 lhsT_scale=scales[:, rows],
                 rhs=w_codes[m][:, cols].bitcast(FP8X4),
@@ -182,12 +147,12 @@ def tile_layernormlstmcell_kernel(
                 stop=True,
             )
 
-        def product_channels(bank, m, g, j):
-            codes, scales = st["codes", m, g // 2]
-            cols = slice(j * P, (j + 1) * P)
-            rows = slice(g % 2 * ROWS, (g % 2 + 1) * ROWS)
+        def product_channels(out, m, g, j):
+            codes, scales = held["codes", m, g // PER_LOAD]
+            first = g % PER_LOAD * ROWS
+            rows, cols = slice(first, first + ROWS), slice(j * P, (j + 1) * P)
             nc.tensor.matmul_mx(
-                out=bank,
+                out=out,
                 lhsT=w_codes[m][:, cols].bitcast(FP8X4),
                 lhsT_scale=w_scales[m][:, cols],
                 rhs=codes[:, rows].bitcast(FP8X4),
@@ -197,109 +162,107 @@ def tile_layernormlstmcell_kernel(
             )
 
         def open_stats(g):
-            st["mean_var", g] = work.tile([P, PAIRS, 2], F32, name="mean_var", bufs=6)
-            st["squares", g] = work.tile([P, TILES, 2], F32, name="squares", bufs=3)
+            held["mean_var", g] = work.tile([P, PAIRS, 2], F32, name="mean_var", bufs=6)
+            held["squares", g] = work.tile([P, TILES, 2], F32, name="squares", bufs=3)
 
         def vector_stats(g, pair, c):
-            if c == 0:
-                st["bn", g, pair] = work.tile([P, CHUNKS, 6], F32, name="bn", bufs=8)
+            if ("bn", g, pair) not in held:
+                held["bn", g, pair] = work.tile([P, CHUNKS, 6], F32, name="bn", bufs=2 * PAIRS)
             bank = vector_bank()
-            product_rows(bank, pair // TILES, g, pair % TILES, c)
-            nc.vector.bn_stats(out=st["bn", g, pair][:, c, :], in_=bank[:])
+            product_rows(bank[:], pair // TILES, g, pair % TILES, c)
+            nc.vector.bn_stats(out=held["bn", g, pair][:, c, :], in_=bank[:])
 
         def vector_stats_end(g, pair):
-            nc.vector.bn_aggr(out=st["mean_var", g][:, pair, :], in_=st["bn", g, pair][:].rearrange("p c s -> p (c s)"))
+            parts = held["bn", g, pair][:].rearrange("p c s -> p (c s)")
+            nc.vector.bn_aggr(out=held["mean_var", g][:, pair, :], in_=parts)
 
         def scalar_sum(g, pair, c):
             if c == 0:
-                st["scaled", g, pair] = work.tile([P, G], F32, name="scaled", bufs=2)
-                st["part", g, pair] = work.tile([P, 2, CHUNKS], F32, name="part", bufs=3)
+                held["scaled", g, pair] = work.tile([P, G], F32, name="scaled")
+                held["part", g, pair] = work.tile([P, 2, CHUNKS], F32, name="part", bufs=3)
             bank = scalar_bank()
-            product_rows(bank, pair // TILES, g, pair % TILES, c)
+            product_rows(bank[:], pair // TILES, g, pair % TILES, c)
             nc.scalar.activation(
-                out=st["scaled", g, pair][:, c * BANK : (c + 1) * BANK],
+                out=held["scaled", g, pair][:, c * BANK : (c + 1) * BANK],
                 in_=bank[:],
                 func=ACT.Copy,
                 scale=1.0 / G,
-                accum_out=st["part", g, pair][:, 0, c : c + 1],
+                accum_out=held["part", g, pair][:, 0, c : c + 1],
             )
 
         def scalar_mean(g, pair):
-            part = st["part", g, pair]
-            nc.scalar.activation(
-                out=part[:, 1, :], in_=part[:, 0, :], func=ACT.Copy, accum_out=st["mean_var", g][:, pair, 0:1]
-            )
+            part = held["part", g, pair]
+            mean = held["mean_var", g][:, pair, 0:1]
+            nc.scalar.activation(out=part[:, 1, :], in_=part[:, 0, :], func=ACT.Copy, accum_out=mean)
 
         def scalar_squares(g, pair, half):
-            scaled = st["scaled", g, pair][:, half * G // 2 : (half + 1) * G // 2]
-            at = pair - TILES
+            scaled = held["scaled", g, pair][:, half * G // 2 : (half + 1) * G // 2]
             nc.scalar.activation(
                 out=scaled,
                 in_=scaled,
                 func=ACT.Square,
                 scale=-float(G),
-                bias=st["mean_var", g][:, pair, 0:1],
-                accum_out=st["squares", g][:, at, half : half + 1],
+                bias=held["mean_var", g][:, pair, 0:1],
+                accum_out=held["squares", g][:, pair % TILES, half : half + 1],
             )
 
         def scalar_var(g, pair):
-            halves = st["squares", g][:, pair - TILES, :]
-            nc.scalar.activation(
-                out=halves, in_=halves, func=ACT.Copy, scale=1.0 / G, accum_out=st["mean_var", g][:, pair, 1:2]
-            )
-
-        small = nc.gpsimd if SMALL == "gpsimd" else nc.vector
+            halves = held["squares", g][:, pair % TILES, :]
+            var = held["mean_var", g][:, pair, 1:2]
+            nc.scalar.activation(out=halves, in_=halves, func=ACT.Copy, scale=1.0 / G, accum_out=var)
 
         def row_rstd(g):
-            mean_var = st["mean_var", g]
+            mean_var = held["mean_var", g]
             var_eps = work.tile([P, PAIRS], F32, name="var_eps", bufs=5)
             rstd = work.tile([P, PAIRS], F32, name="rstd", bufs=5)
-            terms = work.tile([P, PAIRS, 4], F32, name="terms", bufs=5)
-            small.tensor_scalar(var_eps[:], mean_var[:, :, 1], 1.0, EPS, ALU.mult, ALU.add)
+            terms = work.tile([P, PAIRS, TERMS], F32, name="terms", bufs=5)
+            nc.gpsimd.tensor_scalar(var_eps[:], mean_var[:, :, 1], 1.0, EPS, ALU.mult, ALU.add)
             nc.gpsimd.tensor_tensor(rstd[:], var_eps[:], minus_half[:], ALU.pow)
-            small.tensor_scalar(terms[:, :, 2], mean_var[:, :, 0], -1.0, 0.0, ALU.mult, ALU.add)
-            st["rstd", g], st["var_eps", g], st["terms", g] = rstd, var_eps, terms
+            nc.gpsimd.tensor_scalar(terms[:, :, 2], mean_var[:, :, 0], -1.0, 0.0, ALU.mult, ALU.add)
+            held["rstd", g], held["var_eps", g], held["terms", g] = rstd, var_eps, terms
 
         def row_std(g):
-            rstd, var_eps, terms = st["rstd", g], st["var_eps", g], st["terms", g]
             twice = [P, TILES, 2]
-            small.tensor_tensor(
-                terms[:, :TILES, 0:2],
-                var_eps[:, :TILES].unsqueeze(2).to_broadcast(twice),
-                rstd[:, :TILES].unsqueeze(2).to_broadcast(twice),
+            nc.gpsimd.tensor_tensor(
+                held["terms", g][:, :TILES, 0:2],
+                held["var_eps", g][:, :TILES].unsqueeze(2).to_broadcast(twice),
+                held["rstd", g][:, :TILES].unsqueeze(2).to_broadcast(twice),
                 ALU.mult,
             )
 
         def row_ratio(g):
             ratio = work.tile([P, TILES], F32, name="ratio", bufs=5)
-            small.tensor_tensor(ratio[:], st["terms", g][:, :TILES, 0], st["rstd", g][:, TILES:], ALU.mult)
-            st["ratio", g] = ratio
+            nc.gpsimd.tensor_tensor(ratio[:], held["terms", g][:, :TILES, 0], held["rstd", g][:, TILES:], ALU.mult)
+            held["ratio", g] = ratio
 
-        def row_shift(g):
-            terms = st["terms", g]
-            small.tensor_tensor(terms[:, :TILES, 3], terms[:, TILES:, 2], st["ratio", g][:], ALU.mult)
+        def row_mean_hh(g):
+            terms = held["terms", g]
+            nc.gpsimd.tensor_tensor(terms[:, :TILES, 3], terms[:, TILES:, 2], held["ratio", g][:], ALU.mult)
+            held["rest", g] = terms[:, :TILES, :]
+
+        def piece_view(g, i):
+            used = pieces[g % 2][:, :, : TERMS * PIECES]
+            return used.rearrange("p t (v s) -> p t v s", s=PIECES)[:, :, :, i]
 
         def row_piece(g, i):
-            split = pieces[g % 2][:, :, 0:12].rearrange("p t (v s) -> p t v s", s=3)
-            small.tensor_copy(out=split[:, :, :, i], in_=st["rest", g] if i else st["terms", g][:, :TILES, :])
+            nc.gpsimd.tensor_copy(out=piece_view(g, i), in_=held["rest", g])
 
         def row_rest(g, i):
-            split = pieces[g % 2][:, :, 0:12].rearrange("p t (v s) -> p t v s", s=3)
-            rest = work.tile([P, TILES, 4], F32, name="rest", bufs=4)
-            before = st["rest", g] if i else st["terms", g][:, :TILES, :]
-            small.tensor_tensor(rest[:], before, split[:, :, :, i], ALU.subtract)
-            st["rest", g] = rest[:]
+            rest = work.tile([P, TILES, TERMS], F32, name="rest", bufs=4)
+            nc.gpsimd.tensor_tensor(rest[:], held["rest", g], piece_view(g, i), ALU.subtract)
+            held["rest", g] = rest[:]
 
-        chain = [(row_std,), (row_ratio,), (row_shift,), (row_piece, 0), (row_rest, 0), (row_piece, 1), (row_rest, 1), (row_piece, 2)]
+        factor_chain = [(row_std,), (row_ratio,), (row_mean_hh,)]
+        factor_chain += [(row_piece, 0), (row_rest, 0), (row_piece, 1), (row_rest, 1), (row_piece, 2)]
 
         def spread_ratio(g):
             bank = scalar_bank()
             for t in range(TILES):
-                col = st["ratio", g][:, t : t + 1].to_broadcast([P, P])
-                nc.tensor.transpose(bank[:, t * P : (t + 1) * P], col, ident[:])
+                repeated = held["ratio", g][:, t : t + 1].to_broadcast([P, P])
+                nc.tensor.transpose(bank[:, t * P : (t + 1) * P], repeated, ident[:])
             ratio_all = work.tile([P, ROWS], F32, name="ratio_all")
             nc.scalar.copy(out=ratio_all[:], in_=bank[:, :ROWS])
-            st["ratio_all", g] = ratio_all
+            held["ratio_all", g] = ratio_all
 
         def turn_pieces(g):
             bank = scalar_bank(BF16)
@@ -307,368 +270,366 @@ def tile_layernormlstmcell_kernel(
                 nc.tensor.transpose(bank[:, t * P : (t + 1) * P], pieces[g % 2][:, t, :], ident_bf[:])
             shift_lhs = work.tile([P, ROWS], BF16, name="shift_lhs")
             nc.scalar.copy(out=shift_lhs[:], in_=bank[:, :ROWS])
-            st["shift_lhs", g] = shift_lhs
+            held["shift_lhs", g] = shift_lhs
 
-        def channel_block(s, i):
-            n = s * PER_BANK + i
-            return TURNED_GATES[n // 4] * 4 + n % 4
+        def channel_products(bank, m, g, s):
+            found = []
+            for i in range(PER_BANK):
+                q, block = divmod(s * PER_BANK + i, BLOCKS)
+                j = GATE_ORDER[q] * BLOCKS + block
+                cols = bank[:, i * ROWS : (i + 1) * ROWS]
+                product_channels(cols, m, g, j)
+                found.append((cols, gain_cols[:, m * G // P + j : m * G // P + j + 1]))
+            return found
 
-        def scaled_ih(g, s):
-            bank = scalar_bank()
-            u = work.tile([P, PER_BANK, ROWS], F32, name="u_ih", bufs=UB)
-            for i in range(PER_BANK):
-                product_channels(bank[:, i * ROWS : (i + 1) * ROWS], 0, g, channel_block(s, i))
-            for i in range(PER_BANK):
-                j = channel_block(s, i)
-                nc.scalar.activation(
-                    out=u[:, i, :], in_=bank[:, i * ROWS : (i + 1) * ROWS], func=ACT.Copy, scale=gamma_cols[:, j : j + 1]
-                )
-            st["u", 0, g, s] = u
+        def scaled_tile(m):
+            return work.tile([P, PER_BANK, ROWS], F32, name="gained%d" % m, bufs=5)
 
-        def scaled_hh(g, s):
-            bank = vector_bank()
-            u = work.tile([P, PER_BANK, ROWS], F32, name="u_hh", bufs=UB)
-            for i in range(PER_BANK):
-                product_channels(bank[:, i * ROWS : (i + 1) * ROWS], 1, g, channel_block(s, i))
-            for i in range(PER_BANK):
-                j = G // P + channel_block(s, i)
+        def gained_ih(g, s):
+            gained = scaled_tile(IH)
+            for i, (cols, gamma) in enumerate(channel_products(scalar_bank(), IH, g, s)):
+                nc.scalar.activation(out=gained[:, i, :], in_=cols, func=ACT.Copy, scale=gamma)
+            held["gained", IH, g, s] = gained
+
+        def gained_hh(g, s):
+            gained = scaled_tile(HH)
+            for i, (cols, gamma) in enumerate(channel_products(vector_bank(), HH, g, s)):
                 nc.vector.scalar_tensor_tensor(
-                    u[:, i, :],
-                    bank[:, i * ROWS : (i + 1) * ROWS],
-                    gamma_cols[:, j : j + 1],
-                    st["ratio_all", g][:],
-                    ALU.mult,
-                    ALU.mult,
+                    gained[:, i, :], cols, gamma, held["ratio_all", g][:], ALU.mult, ALU.mult
                 )
-            st["u", 1, g, s] = u
+            held["gained", HH, g, s] = gained
+
+        def gate_tile(which):
+            return work.tile([P, H], F32, name="gate%d" % which, bufs=7 if which == GATE_O else 4)
 
         def gate(g, item):
             q, t = divmod(item, TILES)
-            which = TURNED_GATES[q]
+            which = GATE_ORDER[q]
             rows = slice(t * P, (t + 1) * P)
             bank = scalar_bank()
             nc.tensor.matmul(
-                bank[:], st["shift_lhs", g][:, rows], shift_rhs[:, which * H : (which + 1) * H], start=True, stop=False
+                bank[:],
+                held["shift_lhs", g][:, rows],
+                shift_rhs[:, which * H : (which + 1) * H],
+                start=True,
+                stop=False,
             )
-            for m in range(2):
-                for i in range(4):
+            for m in (IH, HH):
+                for i in range(BLOCKS):
+                    s, slot = divmod(BLOCKS * q + i, PER_BANK)
                     nc.tensor.matmul(
                         bank[:, i * P : (i + 1) * P],
-                        st["u", m, g, (4 * q + i) // PER_BANK][:, i % PER_BANK, rows],
+                        held["gained", m, g, s][:, slot, rows],
                         ident[:],
                         start=False,
-                        stop=(m == 1 and i == 3),
+                        stop=(m == HH and i == BLOCKS - 1),
                         is_transpose=True,
                     )
-            value = work.tile([P, H], F32, name="gate%d" % which, bufs=4)
+            value = gate_tile(which)
             func = ACT.Tanh if which == GATE_G else ACT.Sigmoid
-            nc.scalar.activation(out=value[:], in_=bank[:], func=func, scale=st["rstd", g][:, t : t + 1])
-            st["gate", which, g, t] = value
+            nc.scalar.activation(out=value[:], in_=bank[:], func=func, scale=held["rstd", g][:, t : t + 1])
+            held["gate", which, g, t] = value
 
         def o_centred(g, t, m):
             bank = vector_bank()
-            product_rows(bank, m, g, t, GATE_O)
-            u = work.tile([P, H], F32, name="o_part%d" % m, bufs=3)
-            mean = st["mean_var", g][:, m * TILES + t, 0:1]
-            nc.vector.scalar_tensor_tensor(u[:], bank[:], mean, gamma_o[m][:], ALU.subtract, ALU.mult)
-            st["o_part", m, g, t] = u
+            product_rows(bank[:], m, g, t, GATE_O)
+            part = work.tile([P, H], F32, name="o_part%d" % m, bufs=3)
+            mean = held["mean_var", g][:, m * TILES + t, 0:1]
+            nc.vector.scalar_tensor_tensor(part[:], bank[:], mean, gamma_o[m][:], ALU.subtract, ALU.mult)
+            held["o_part", m, g, t] = part
 
         def o_sum(g, t):
-            u = st["o_part", 1, g, t]
-            ratio = st["ratio", g][:, t : t + 1]
-            nc.vector.scalar_tensor_tensor(u[:], u[:], ratio, st["o_part", 0, g, t][:], ALU.mult, ALU.add)
+            total, ratio = held["o_part", HH, g, t], held["ratio", g][:, t : t + 1]
+            nc.vector.scalar_tensor_tensor(total[:], total[:], ratio, held["o_part", IH, g, t][:], ALU.mult, ALU.add)
 
         def o_bias(g, t):
-            u = st["o_part", 1, g, t]
-            nc.vector.scalar_tensor_tensor(u[:], beta_o[:], st["terms", g][:, t, 0:1], u[:], ALU.mult, ALU.add)
+            total, std = held["o_part", HH, g, t], held["terms", g][:, t, 0:1]
+            nc.vector.scalar_tensor_tensor(total[:], beta_o[:], std, total[:], ALU.mult, ALU.add)
 
         def o_gate(g, t):
-            value = work.tile([P, H], F32, name="gate_o", bufs=6)
-            nc.scalar.activation(
-                out=value[:], in_=st["o_part", 1, g, t][:], func=ACT.Sigmoid, scale=st["rstd", g][:, t : t + 1]
-            )
-            st["gate", GATE_O, g, t] = value
+            value = gate_tile(GATE_O)
+            rstd = held["rstd", g][:, t : t + 1]
+            nc.scalar.activation(out=value[:], in_=held["o_part", HH, g, t][:], func=ACT.Sigmoid, scale=rstd)
+            held["gate", GATE_O, g, t] = value
+
+        def cell_engine(g):
+            return nc.vector if g == LAST else nc.gpsimd
+
+        def tile_rows(g, t):
+            return slice((g * TILES + t) * P, (g * TILES + t + 1) * P)
 
         def input_term(g, t):
-            i_gate = st["gate", GATE_I, g, t]
-            (nc.gpsimd if T1POOL and g < VEC_FROM + 1 else nc.vector).tensor_tensor(i_gate[:], i_gate[:], st["gate", GATE_G, g, t][:], ALU.mult)
-            st["input_term", g, t] = i_gate
+            i_gate = held["gate", GATE_I, g, t]
+            cell_engine(g).tensor_tensor(i_gate[:], i_gate[:], held["gate", GATE_G, g, t][:], ALU.mult)
 
-        def cell(g, t):
-            f_gate = st["gate", GATE_F, g, t]
-            c_new = work.tile([P, H], F32, name="c_new", bufs=4)
-            engine = nc.vector if g >= VEC_FROM or not T2POOL else nc.gpsimd
-            engine.tensor_tensor(f_gate[:], f_gate[:], st["c_prev", g // 2][:, g % 2 * TILES + t, :], ALU.mult)
-            st["c", g, t] = c_new
+        def forget_term(g, t):
+            f_gate = held["gate", GATE_F, g, t]
+            c_old = held["c_prev", g // PER_LOAD][:, g % PER_LOAD * TILES + t, :]
+            cell_engine(g).tensor_tensor(f_gate[:], f_gate[:], c_old, ALU.mult)
 
         def cell_sum(g, t):
-            f_gate = st["gate", GATE_F, g, t]
-            c_new = st["c", g, t]
-            engine = nc.vector if g >= VEC_FROM else nc.gpsimd
-            if SUMV:
-                total = work.tile([P, 4], F32, name="c_total", bufs=3)
-                nc.vector.scalar_tensor_tensor(c_new[:], f_gate[:], 1.0, st["input_term", g, t][:], ALU.mult, ALU.add, accum_out=total[:, 0:1])
-                st["c_total", g, t] = total
-            else:
-                engine.tensor_tensor(c_new[:], f_gate[:], st["input_term", g, t][:], ALU.add)
-            row = (g * TILES + t) * P
-            nc.sync.dma_start(out=out_1[row : row + P, :], in_=c_new[:])
+            c_new = work.tile([P, H], F32, name="c_new", bufs=4)
+            terms = held["gate", GATE_F, g, t], held["gate", GATE_I, g, t]
+            cell_engine(g).tensor_tensor(c_new[:], terms[0][:], terms[1][:], ALU.add)
+            nc.sync.dma_start(out=out_1[tile_rows(g, t), :], in_=c_new[:])
+            held["c", g, t] = c_new
 
         def cell_stats(g, t):
-            if SUMV:
-                mean_var = work.tile([P, 2], F32, name="c_mean_var", bufs=3)
-                st["c_mean", g, t] = mean_var
-                nc.scalar.activation(out=mean_var[:, 0:1], in_=st["c_total", g, t][:, 0:1], func=ACT.Copy, scale=1.0 / H)
-                return
             bn = work.tile([P, 6], F32, name="c_bn")
-            nc.vector.bn_stats(out=bn[:], in_=st["c", g, t][:])
-            st["c_bn", g, t] = bn
+            nc.vector.bn_stats(out=bn[:], in_=held["c", g, t][:])
+            held["c_bn", g, t] = bn
 
         def cell_mean(g, t):
-            if SUMV:
-                mean_var = st["c_mean", g, t]
-                junk = work.tile([P, H], F32, name="c_squares")
-                nc.scalar.activation(out=junk[:], in_=st["c", g, t][:], func=ACT.Square, scale=-1.0, bias=mean_var[:, 0:1], accum_out=mean_var[:, 1:2])
-                return
             mean_var = work.tile([P, 2], F32, name="c_mean_var", bufs=3)
-            nc.vector.bn_aggr(out=mean_var[:], in_=st["c_bn", g, t][:])
-            st["c_mean", g, t] = mean_var
+            nc.vector.bn_aggr(out=mean_var[:], in_=held["c_bn", g, t][:])
+            held["c_mean_var", g, t] = mean_var
+
+        def cell_var(g, t):
+            var_eps = work.tile([P, 1], F32, name="c_var_eps", bufs=3)
+            nc.gpsimd.tensor_scalar(var_eps[:], held["c_mean_var", g, t][:, 1:2], 1.0, EPS, ALU.mult, ALU.add)
+            held["c_var_eps", g, t] = var_eps
 
         def cell_rstd(g, t):
-            mean_var = st["c_mean", g, t]
-            var_eps = work.tile([P, 1], F32, name="c_var_eps", bufs=3)
             rstd = work.tile([P, 1], F32, name="c_rstd", bufs=3)
-            small.tensor_scalar(var_eps[:], mean_var[:, 1:2], 1.0 / H if SUMV else 1.0, EPS, ALU.mult, ALU.add)
-            nc.gpsimd.tensor_tensor(rstd[:], var_eps[:], minus_half[:, 0:1], ALU.pow)
-            st["c_rstd", g, t] = rstd
-            if NACT:
-                shift = work.tile([P, 1], F32, name="c_shift", bufs=3)
-                small.tensor_scalar(shift[:], mean_var[:, 0:1], rstd[:], minus_one, ALU.mult, ALU.mult)
-                st["c_shift", g, t] = shift
+            nc.gpsimd.tensor_tensor(rstd[:], held["c_var_eps", g, t][:], minus_half[:, 0:1], ALU.pow)
+            held["c_rstd", g, t] = rstd
+
+        def cell_rstd_at_once(g, t):
+            cell_rstd(g, t)
 
         def cell_normed(g, t):
-            y = work.tile([P, H], F32, name="c_norm", bufs=3)
-            mean = st["c_mean", g, t][:, 0:1]
-            if NACT:
-                nc.scalar.activation(out=y[:], in_=st["c", g, t][:], func=ACT.Identity, scale=st["c_rstd", g, t][:], bias=st["c_shift", g, t][:])
-            else:
-                nc.vector.tensor_scalar(y[:], st["c", g, t][:], mean, st["c_rstd", g, t][:], ALU.subtract, ALU.mult)
-            st["c_norm", g, t] = y
+            normed = work.tile([P, H], F32, name="c_normed", bufs=4)
+            mean, rstd = held["c_mean_var", g, t][:, 0:1], held["c_rstd", g, t][:]
+            nc.vector.tensor_scalar(normed[:], held["c", g, t][:], mean, rstd, ALU.subtract, ALU.mult)
+            held["c_normed", g, t] = normed
+
+        def turn_tile(bank, src):
+            for i in range(BLOCKS):
+                nc.tensor.transpose(bank[:, i * P : (i + 1) * P], src[:, i * P : (i + 1) * P], ident[:])
 
         def cell_tanh(g, t):
-            y = st["c_norm", g, t]
             bank = scalar_bank()
-            for i in range(4):
-                nc.tensor.transpose(bank[:, i * P : (i + 1) * P], y[:, i * P : (i + 1) * P], ident[:])
-            z = work.tile([P, H], F32, name="c_tanh", bufs=3)
-            for i in range(4):
+            turn_tile(bank, held["c_normed", g, t])
+            c_tanh = work.tile([P, H], F32, name="c_tanh", bufs=4)
+            for i in range(BLOCKS):
                 nc.scalar.activation(
-                    out=z[:, i * P : (i + 1) * P],
+                    out=c_tanh[:, i * P : (i + 1) * P],
                     in_=bank[:, i * P : (i + 1) * P],
                     func=ACT.Tanh,
-                    scale=gamma_cols[:, 32 + i : 33 + i],
-                    bias=gamma_cols[:, 36 + i : 37 + i],
+                    scale=gain_cols[:, NORM_COL + i : NORM_COL + i + 1],
+                    bias=gain_cols[:, NORM_COL + BLOCKS + i : NORM_COL + BLOCKS + i + 1],
                 )
-            st["c_tanh", g, t] = z
+            held["c_tanh", g, t] = c_tanh
 
         def hidden(g, t):
-            z = st["c_tanh", g, t]
             bank = vector_bank()
-            for i in range(4):
-                nc.tensor.transpose(bank[:, i * P : (i + 1) * P], z[:, i * P : (i + 1) * P], ident[:])
+            turn_tile(bank, held["c_tanh", g, t])
             h_new = work.tile([P, H], F32, name="h_new", bufs=3)
-            nc.vector.tensor_tensor(h_new[:], bank[:], st["gate", GATE_O, g, t][:], ALU.mult)
-            row = (g * TILES + t) * P
-            nc.sync.dma_start(out=out_0[row : row + P, :], in_=h_new[:])
+            nc.vector.tensor_tensor(h_new[:], bank[:], held["gate", GATE_O, g, t][:], ALU.mult)
+            nc.sync.dma_start(out=out_0[tile_rows(g, t), :], in_=h_new[:])
 
-        def pool_copy(out, in_):
-            nc.gpsimd.tensor_scalar(out, in_, 1.0, 0.0, ALU.mult, ALU.add)
+        def head_stats(m, c):
+            for t in range(TILES):
+                vector_stats(0, m * TILES + t, c)
 
-        def vector_pairs(g):
-            return list(range(PAIRS - SCALAR_PAIRS[g]))
-
-        def scalar_pairs(g):
-            return list(range(PAIRS - SCALAR_PAIRS[g], PAIRS))
-
-        load_weight(0, 0)
-        load_act(0, 0)
-        load_weight(0, 1)
-        load_weight(0, 2)
-        load_act(1, 0)
-        load_weight(0, 3)
+        load_weight(IH, 0)
+        load_input(IH, 0)
+        load_weight(IH, 1)
+        load_weight(IH, 2)
+        load_input(HH, 0)
+        load_weight(IH, 3)
         make_identity(nc, ident[:])
         make_identity(nc, ident_bf[:])
-        nc.gpsimd.memset(gamma_rows[:], 0.0)
+        nc.gpsimd.memset(gain_rows[:], 0.0)
         nc.gpsimd.memset(shift_rhs[:], 0.0)
         nc.gpsimd.memset(minus_half[:], -0.5)
-        for i in range(2):
-            nc.gpsimd.memset(pieces[i][:], 0.0)
+        for tile in pieces:
+            nc.gpsimd.memset(tile[:], 0.0)
         open_stats(0)
-        open_stats(1)
-        ih_tiles = [(g, t) for g in range(2) for t in range(TILES)]
 
-        def head_stats(c, first, last):
-            for g, t in ih_tiles[first:last]:
-                vector_stats(g, t, c)
+        interleave_weight(IH, 0, nc.vector.tensor_copy)
+        load_weight(HH, 0)
+        turn_input(IH, 0, 0)
+        turn_input(IH, 0, 1)
+        load_weight(HH, 1)
+        quantize_weight(IH, 0)
+        interleave_weight(IH, 1, nc.scalar.copy)
+        load_weight(HH, 2)
+        quantize_input(IH, 0)
+        interleave_weight(IH, 2, nc.vector.tensor_copy)
+        load_weight(HH, 3)
+        vector_stats(0, 0, 0)
+        quantize_weight(IH, 2)
+        quantize_weight(IH, 1)
+        turn_input(HH, 0, 0)
+        turn_input(HH, 0, 1)
+        load_input(IH, 1)
+        vector_stats(0, 1, 0)
+        head_stats(IH, 2)
+        quantize_input(HH, 0)
+        interleave_weight(IH, 3, nc.scalar.copy)
+        load_input(HH, 1)
+        interleave_weight(HH, 0, nc.vector.tensor_copy)
+        vector_stats(0, 0, 1)
+        quantize_weight(HH, 0)
+        quantize_weight(IH, 3)
+        interleave_weight(HH, 1, nc.scalar.copy)
+        interleave_weight(HH, 2, nc.vector.tensor_copy)
+        vector_stats(0, 1, 1)
+        quantize_weight(HH, 2)
+        quantize_weight(HH, 1)
+        interleave_weight(HH, 3, nc.scalar.copy)
+        head_stats(IH, 3)
+        head_stats(HH, 0)
+        quantize_weight(HH, 3)
 
-        interleave_weight(0, 0, nc.vector.tensor_copy)
-        load_weight(1, 0)
-        turn_act(0, 0, 0)
-        turn_act(0, 0, 1)
-        load_weight(1, 1)
-        quantize_weight(0, 0)
-        interleave_weight(0, 1, nc.scalar.copy)
-        load_weight(1, 2)
-        quantize_act(0, 0)
-        interleave_weight(0, 2, nc.vector.tensor_copy)
-        load_weight(1, 3)
-        head_stats(0, 0, 1)
-        quantize_weight(0, 2)
-        quantize_weight(0, 1)
-        turn_act(1, 0, 0)
-        turn_act(1, 0, 1)
-        load_act(0, 1)
-        head_stats(0, 1, 3)
-        quantize_act(1, 0)
-        interleave_weight(0, 3, nc.scalar.copy)
-        load_act(1, 1)
-        interleave_weight(1, 0, nc.vector.tensor_copy)
-        head_stats(0, 3, 4)
-        quantize_weight(1, 0)
-        quantize_weight(0, 3)
-        interleave_weight(1, 1, nc.scalar.copy)
-        interleave_weight(1, 2, nc.vector.tensor_copy)
-        head_stats(1, 0, 1)
-        quantize_weight(1, 2)
-        quantize_weight(1, 1)
-        interleave_weight(1, 3, nc.scalar.copy)
-        head_stats(1, 1, 2)
-        head_stats(2, 0, 2)
-        quantize_weight(1, 3)
-        for m, gamma in enumerate((gamma_ih, gamma_hh)):
-            nc.sync.dma_start(
-                out=gamma_rows[m * G // P : (m + 1) * G // P, :], in_=gamma.rearrange("(j n) -> j n", n=P)
-            )
-        if True:
-            for m, vec in enumerate((gamma_c, beta_c)):
-                nc.sync.dma_start(out=gamma_rows[32 + 4 * m : 36 + 4 * m, :], in_=vec.rearrange("(j n) -> j n", n=P))
+        row = 0
+        for vec in (gamma_ih, gamma_hh, gamma_c, beta_c):
+            blocks = vec.shape[0] // P
+            nc.sync.dma_start(out=gain_rows[row : row + blocks, :], in_=vec.rearrange("(j n) -> j n", n=P))
+            row += blocks
         for v, vec in enumerate((beta_ih, beta_hh, gamma_ih, gamma_hh)):
-            nc.sync.dma_start(out=shift_rhs[3 * v : 3 * v + 3, :], in_=vec[: GATE_O * H].partition_broadcast(3))
+            nc.sync.dma_start(out=shift_rhs[PIECES * v : PIECES * (v + 1), :], in_=vec.partition_broadcast(PIECES))
         for dst, vec in zip(gamma_o + beta_o_parts, (gamma_ih, gamma_hh, beta_ih, beta_hh)):
             nc.sync.dma_start(out=dst[:], in_=vec[GATE_O * H :].partition_broadcast(P))
-        vector_list = [(vector_stats, 0, t, 3) for t in range(TILES)]
-        vector_list += [(vector_stats, 0, TILES + t, c) for t in range(TILES) for c in range(CHUNKS)]
-        vector_list += [(vector_stats_end, 0, pair) for pair in range(PAIRS)] + [(row_rstd, 0)]
-        rest_of_ih = [(vector_stats, 1, t, c) for t in range(TILES) for c in range(1, CHUNKS)]
-        for n, entry in enumerate(chain):
-            vector_list += rest_of_ih[n : n + 1] + [(entry[0], 0) + entry[1:]]
-        vector_list += [(vector_stats_end, 1, t) for t in range(TILES)]
-        scalar_list = []
-        for pair in scalar_pairs(1):
-            m = pair - TILES
-            scalar_list += [(scalar_sum, 1, pair, c) for c in range(CHUNKS)]
-            scalar_list += [(scalar_mean, 1, pair)]
-            scalar_list += [(turn_act, m, 1, 0), (turn_act, m, 1, 1), (quantize_act, m, 1)]
-            scalar_list += [(scalar_squares, 1, pair, 0), (scalar_squares, 1, pair, 1), (scalar_var, 1, pair)]
-        nc.gpsimd.tensor_tensor(beta_o[:], beta_o_parts[0][:], beta_o_parts[1][:], ALU.add)
-        taken = 0
-        for n, entry in enumerate(scalar_list):
-            entry[0](*entry[1:])
-            while taken < len(vector_list) * (n + 1) // len(scalar_list):
-                vector_list[taken][0](*vector_list[taken][1:])
-                taken += 1
-        bank = scalar_bank(BF16)
-        nc.tensor.transpose(bank[:, :P], gamma_rows[:], ident_bf[:])
-        nc.scalar.copy(out=gamma_cols[:], in_=bank[:, :40])
+        nc.gpsimd.tensor_tensor(beta_o[:], beta_o_parts[IH][:], beta_o_parts[HH][:], ALU.add)
+        gain_bank = scalar_bank(BF16)
+        nc.tensor.transpose(gain_bank[:, :P], gain_rows[:], ident_bf[:])
+        nc.scalar.copy(out=gain_cols[:], in_=gain_bank[:, : NORM_COL + 2 * BLOCKS])
 
+        for_vector = (gained_hh, o_centred, vector_stats)
+        for_scalar = (gained_ih, scalar_sum)
+        then = [open_stats, load_input, cell_stats, o_gate, scalar_var, scalar_squares]
+        then += [input_term, forget_term, cell_sum, cell_rstd, o_sum, cell_normed, o_bias, cell_mean, cell_var]
+        then += [cell_rstd_at_once, load_cell, quantize_input, vector_stats_end, scalar_mean, row_rstd]
+        then += [entry[0] for entry in factor_chain[:5]]
+        then += [gate, spread_ratio, turn_pieces, turn_input, cell_tanh, hidden]
+        factor_rank = then.index(row_std)
+        whole_passes = (gained_hh, o_centred, o_sum, o_bias, cell_stats, hidden, quantize_input, vector_stats)
+        vector_passes = {fn: 1 for fn in whole_passes}
+        vector_passes[cell_normed] = 0.5
         plan = {}
-        passes = {}
+        ending = {}
 
-        def at(step, rank, fn, *args, vector_passes=0):
-            plan.setdefault(step, []).append((rank, fn, args))
-            passes[step] = passes.get(step, 0) + vector_passes
+        def at(step, fn, *args):
+            plan.setdefault(step, []).append((fn, args))
 
-        VECTOR, SCALAR, SBUF_WORK, LATE, TRANSPOSES = 0, 1, 2, 3, 4
-        for g in range(GROUPS):
-            base = STEPS * g + FIRST
-            if g > 0:
-                at(base - CHAIN, LATE, row_rstd, g)
-                for n, entry in enumerate(chain):
-                    at(base - CHAIN + COFF + n // CPER, RCH, entry[0], g, *entry[1:])
-            at(base - 1, TRANSPOSES, spread_ratio, g)
-            at(base + PT - 1, TRANSPOSES, turn_pieces, g)
-            if g % 2 == 0:
-                at(base, LATE, load_rows, "c_prev", c_prev, g // 2, "c_prev", 2)
-            for s in range(STEPS):
-                at(base + s, SCALAR, scaled_ih, g, s)
-                at(base + s, VECTOR, scaled_hh, g, s, vector_passes=1)
-                at(base + s + SUM_LAG, TRANSPOSES, gate, g, s)
+        def passes(step):
+            return sum(vector_passes.get(fn, 0) for fn, args in plan.get(step, []))
+
+        for c in range(1, CHUNKS):
             for t in range(TILES):
-                done = base + 2 * TILES + SUM_LAG + t * (CELL_GAP if g + 1 < GROUPS else LAST_CELL_GAP)
-                at(done + C1, 2.05, input_term, g, t, vector_passes=1 - T1POOL)
-                at(done + C1, 2.06, cell, g, t, vector_passes=1 - T2POOL)
-                at(done + C2, RS, cell_sum, g, t, vector_passes=SUMV)
-                at(done + C2 + SA, RA, cell_stats, g, t, vector_passes=1 - SUMV)
-                at(done + C2 + SB_, RB, cell_mean, g, t)
-                at(done + C2 + SC, RC, cell_rstd, g, t)
-                at(done + C2 + SD, 2.2, cell_normed, g, t, vector_passes=0.5 - 0.5 * NACT)
-                at(done + C2 + SF, 4.1, cell_tanh, g, t)
-                at(done + C2 + SH, 4.2, hidden, g, t, vector_passes=1)
-                first = done + C2 + SO if g < OJIT else base + CELL_GAP * t + OFF
-                at(first - 1, VECTOR, o_centred, g, t, 0, vector_passes=1)
-                at(first - 1, VECTOR, o_centred, g, t, 1, vector_passes=1)
-                at(first, 2.1, o_sum, g, t, vector_passes=1)
-                at(first, RV2, o_bias, g, t, vector_passes=1)
-                at(first + OG, ROG, o_gate, g, t)
-        ready = {1: 0}
-        for j in range(2, GROUPS // 2):
-            begin = TURN + (2 * STEPS + 1) * (j - 2)
-            for m in range(2):
-                at(begin - 4, SBUF_WORK, load_act, m, j)
-                at(begin + 2 * m, TRANSPOSES, turn_act, m, j, 0)
-                at(begin + 1 + 2 * m, TRANSPOSES, turn_act, m, j, 1)
-                at(begin + 3 + 2 * m, SBUF_WORK, quantize_act, m, j, vector_passes=1)
-            ready[j] = begin + 6
+                at(0, vector_stats, 0, HH * TILES + t, c)
+        for pair in range(PAIRS):
+            at(0, vector_stats_end, 0, pair)
+        at(0, row_rstd, 0)
+        for link in factor_chain:
+            at(1, link[0], 0, *link[1:])
+
+        for g in range(GROUPS):
+            base = PERIOD * g + FIRST
+            if g > 0:
+                at(base - FACTOR_LEAD, row_rstd, g)
+                for n, link in enumerate(factor_chain):
+                    at(base - FACTOR_LEAD + n // 2, link[0], g, *link[1:])
+            at(base - 2 if g > 0 else base - 1, spread_ratio, g)
+            at(base + 1, turn_pieces, g)
+            if g % PER_LOAD == 0:
+                at(base, load_cell, g // PER_LOAD)
+            for s in range(PERIOD + TILES if g == LAST else PERIOD):
+                at(base + s, gained_hh, g, s)
+                at(base + s, gained_ih, g, s)
+                at(base + s + TILES, gate, g, s)
+            if g == LAST:
+                continue
+            for t in range(TILES):
+                done = base + PERIOD + TILE_GAP * t
+                for fn in (input_term, forget_term, cell_sum):
+                    at(done + 1, fn, g, t)
+                for fn in (cell_stats, cell_mean, cell_var):
+                    at(done + TILE_GAP, fn, g, t)
+                if (g, t) == (LAST - 1, TILES - 1):
+                    at(done + TILE_GAP, cell_rstd_at_once, g, t)
+                    normed_at = done + TILE_GAP + 1
+                else:
+                    at(done + TILE_GAP + 1, cell_rstd, g, t)
+                    normed_at = done + 2 * TILE_GAP
+                for n, fn in enumerate((cell_normed, cell_tanh, hidden)):
+                    at(normed_at + n, fn, g, t)
+                o_at = base + TILE_GAP * (t + 1)
+                at(o_at - 1, o_centred, g, t, IH)
+                at(o_at - 1, o_centred, g, t, HH)
+                at(o_at, o_sum, g, t)
+                at(o_at, o_bias, g, t)
+                at(o_at + 1, o_gate, g, t)
+
+        f_done = PERIOD * LAST + FIRST + PERIOD
+        for t in range(TILES):
+            at(f_done - 1 + t, input_term, LAST, t)
+        ending[f_done] = [(fn, 0) for fn in (forget_term, cell_sum, cell_stats, cell_mean, cell_var, cell_rstd)]
+        ending[f_done + 1] = [(forget_term, 1), (cell_normed, 0)]
+        ending[f_done + 1] += [(fn, 1) for fn in (cell_sum, cell_stats, cell_mean, cell_var, cell_rstd)]
+        ending[f_done + 2] = [(cell_normed, 1), (cell_tanh, 0), (hidden, 0)]
+        ending[f_done + 3] = [(cell_tanh, 1), (hidden, 1)]
+
+        ready = {0: 0}
+        for load in range(1, B // (LOAD_TILES * P)):
+            begin = 4 * (load - 1)
+            for m in (IH, HH):
+                if load > 1:
+                    at(begin - 4, load_input, m, load)
+                at(begin + 2 * m, turn_input, m, load, 0)
+                at(begin + 2 * m + 1, turn_input, m, load, 1)
+                at(begin + 2 * m + 2, quantize_input, m, load)
+            ready[load] = begin + 5
+
         opened = {}
-        first = SFIRST
-        for g in range(2, GROUPS):
-            for pair in scalar_pairs(g):
-                opened.setdefault(g, first)
-                assert first >= ready[g // 2]
+        vector_work = []
+        free = 0
+        for g in range(1, GROUPS):
+            free = max(free, ready[g // PER_LOAD])
+            opened[g] = free
+            taken = min(TILES, (PERIOD * g + FIRST - FACTOR_LEAD - free) // SCALAR_SPAN)
+            for pair in range(PAIRS - taken, PAIRS):
                 for c in range(CHUNKS):
-                    at(first + c // 2, SCALAR, scalar_sum, g, pair, c)
-                at(first + 1, LATE, scalar_mean, g, pair)
-                at(first + 2, SBUF_WORK, scalar_squares, g, pair, 0)
-                at(first + PSPAN - 1, 2.5, scalar_squares, g, pair, 1)
-                at(first + PSPAN, 2.0, scalar_var, g, pair)
-                first += PSPAN
-            assert first <= STEPS * g + FIRST - CHAIN, (g, first)
-        todo = [(g, pair, c) for g in range(2, GROUPS) for pair in vector_pairs(g) for c in range(CHUNKS)]
-        end = STEPS * (GROUPS - 1) + FIRST - CHAIN
-        total = len(todo) + sum(passes.get(s, 0) for s in range(end))
+                    at(free + c // 2, scalar_sum, g, pair, c)
+                at(free + 1, scalar_mean, g, pair)
+                at(free + 2, scalar_squares, g, pair, 0)
+                at(free + 3, scalar_squares, g, pair, 1)
+                at(free + SCALAR_SPAN, scalar_var, g, pair)
+                free += SCALAR_SPAN
+            vector_work += [(g, pair, c) for pair in range(PAIRS - taken) for c in range(CHUNKS)]
+        stats_steps = range(1, PERIOD * LAST + FIRST - FACTOR_LEAD)
+        total = len(vector_work) + sum(passes(step) for step in stats_steps)
         spent = 0
-        taken = 0
-        for s in range(end):
-            spent += passes.get(s, 0)
-            while taken < len(todo):
-                g, pair, c = todo[taken]
-                due = STEPS * g + FIRST - CHAIN - 1
-                if (spent >= total * (s + 1) // end and s < due) or s < ready[g // 2]:
+        placed = 0
+        for step in stats_steps:
+            spent += passes(step)
+            while placed < len(vector_work):
+                g, pair, c = vector_work[placed]
+                due = PERIOD * g + FIRST - FACTOR_LEAD - 1
+                ahead = spent >= total * step // len(stats_steps)
+                if (ahead and step < due) or step < ready[g // PER_LOAD]:
                     break
-                taken += 1
-                opened[g] = min(opened.get(g, s), s)
-                at(s, VECTOR, vector_stats, g, pair, c)
-                spent += 1
+                opened[g] = min(opened[g], step)
+                at(step, vector_stats, g, pair, c)
                 if c == CHUNKS - 1:
-                    at(s, LATE, vector_stats_end, g, pair)
-        for g in range(2, GROUPS):
-            at(opened[g] - 1, SBUF_WORK, open_stats, g)
+                    at(step, vector_stats_end, g, pair)
+                placed += 1
+                spent += 1
+        for g in range(1, GROUPS):
+            at(opened[g] - 1, open_stats, g)
+
         for step in sorted(plan):
-            for_vector = [e for e in plan[step] if e[0] == VECTOR]
-            for_scalar = [e for e in plan[step] if e[0] == SCALAR]
+            vector_banks = [e for e in plan[step] if e[0] in for_vector]
+            scalar_banks = [e for e in plan[step] if e[0] in for_scalar]
             order = []
-            for i in range(max(len(for_vector), len(for_scalar))):
-                order += for_vector[i : i + 1] + for_scalar[i : i + 1]
-            order += sorted((e for e in plan[step] if e[0] > SCALAR), key=lambda e: e[0])
-            for rank, fn, args in order:
+            for i in range(max(len(vector_banks), len(scalar_banks))):
+                order += vector_banks[i : i + 1] + scalar_banks[i : i + 1]
+            others = [e for e in plan[step] if e[0] in then]
+            chained = [entry[0] for entry in factor_chain]
+            order += sorted(others, key=lambda e: factor_rank if e[0] in chained else then.index(e[0]))
+            for fn, args in order:
                 fn(*args)
+            for fn, t in ending.get(step, []):
+                fn(LAST, t)

from contextlib import ExitStack

import concourse.mybir as mybir
from concourse.masks import make_identity

B, K, H = 2048, 512, 512
G = 4 * H
EPS = 1e-5
FLOPS = 2 * 2 * B * K * G

F32 = mybir.dt.float32
BF16 = mybir.dt.bfloat16
U32 = mybir.dt.uint32
U8 = mybir.dt.uint8
FP8X4 = mybir.dt.float8_e5m2_x4
ALU = mybir.AluOpType
ACT = mybir.ActivationFunctionType

P = 128
PACK = 4
BANK = 512
CHUNKS = G // BANK
BLOCKS = H // P
IH, HH = 0, 1
GATE_I, GATE_F, GATE_G, GATE_O = 0, 1, 2, 3
GATE_ORDER = (GATE_I, GATE_G, GATE_F, GATE_O)

LOAD_TILES = 4
TILES = 2
ROWS = TILES * P
GROUPS = B // ROWS
LAST = GROUPS - 1
PER_LOAD = LOAD_TILES // TILES
PER_BANK = BANK // ROWS
PAIRS = 2 * TILES
TERMS, PIECES = 4, 3
NORM_COL = 2 * G // P

PERIOD = 3 * TILES
TILE_GAP = PERIOD // TILES
FIRST = 3
FACTOR_LEAD = 4
SCALAR_SPAN = 4


def tile_layernormlstmcell_kernel(
    tc, x, h_prev, c_prev, W_ih, W_hh, gamma_ih, beta_ih, gamma_hh, beta_hh, gamma_c, beta_c, out_0, out_1
):
    nc = tc.nc
    row_inputs = (x, h_prev)
    weights = (W_ih, W_hh)

    with ExitStack() as ctx:
        keep = ctx.enter_context(tc.tile_pool(name="keep", bufs=1))
        work = ctx.enter_context(tc.tile_pool(name="work", bufs=2))
        psum = ctx.enter_context(tc.psum_pool(name="psum", bufs=4))
        ctx.enter_context(tc.manual_schedule())

        def vector_bank():
            return psum.tile([P, BANK], F32, name="vector_bank", tag="vector_bank")

        def scalar_bank(dtype=F32):
            return psum.tile([P, BANK], dtype, name="scalar_bank", tag="scalar_bank")

        ident = keep.tile([P, P], F32, name="ident")
        ident_bf = keep.tile([P, P], BF16, name="ident_bf")
        w_codes = [keep.tile([P, G], U32, name="w_codes%d" % m, align_bytes=64) for m in (IH, HH)]
        w_scales = [keep.tile([P, G], U8, name="w_scales%d" % m, align_bytes=64) for m in (IH, HH)]
        gain_rows = keep.tile([P, P], BF16, name="gain_rows")
        gain_cols = keep.tile([P, NORM_COL + 2 * BLOCKS], F32, name="gain_cols")
        shift_rhs = keep.tile([P, G], BF16, name="shift_rhs")
        pieces = [keep.tile([P, TILES, P], BF16, name="pieces%d" % i) for i in range(2)]
        gamma_o = [keep.tile([P, H], BF16, name="gamma_o%d" % m) for m in (IH, HH)]
        beta_o_parts = [keep.tile([P, H], BF16, name="beta_o_part%d" % m) for m in (IH, HH)]
        beta_o = keep.tile([P, H], F32, name="beta_o")
        minus_half = keep.tile([P, PAIRS], F32, name="minus_half")

        held = {}

        def load_rows(src, load, tag, bufs):
            raw = work.tile([P, LOAD_TILES, K], BF16, name=tag, tag=tag, bufs=bufs)
            rows = src[load * LOAD_TILES * P : (load + 1) * LOAD_TILES * P, :]
            nc.sync.dma_start(out=raw[:], in_=rows.rearrange("(t p) k -> p t k", p=P))
            return raw

        def load_input(m, load):
            held["raw", m, load] = load_rows(row_inputs[m], load, "raw", 6)

        def load_cell(load):
            held["c_prev", load] = load_rows(c_prev, load, "c_prev", 2)

        def load_weight(m, c):
            raw = work.tile([P, PACK, BANK], BF16, name="raw", tag="raw", bufs=6)
            cols = weights[m][:, c * BANK : (c + 1) * BANK]
            nc.sync.dma_start(out=raw[:], in_=cols.rearrange("(p j) n -> p j n", j=PACK))
            held["w_raw", m, c] = raw

        def grouped_tile():
            return work.tile([P, BANK * PACK], BF16, name="grouped", tag="grouped", bufs=4, align_bytes=64)

        def interleave_weight(m, c, copy):
            grouped = grouped_tile()
            copy(
                out=grouped[:].rearrange("p (n i j) -> p n j i", i=4, j=PACK),
                in_=held["w_raw", m, c][:].rearrange("p j (n i) -> p n j i", i=4),
            )
            held["w_grouped", m, c] = grouped

        def quantize_weight(m, c):
            cols = slice(c * BANK, (c + 1) * BANK)
            nc.vector.quantize_mx(
                out=w_codes[m][:, cols].bitcast(FP8X4), scales=w_scales[m][:, cols], in_=held["w_grouped", m, c][:]
            )

        def turn_input(m, load, half):
            if half == 0:
                held["grouped", m, load] = grouped_tile()
            bank = scalar_bank()
            for i in range(2):
                words = held["raw", m, load][:, 2 * half + i, :].bitcast(F32)
                for u in range(2):
                    col = (2 * i + u) * P
                    nc.tensor.transpose(bank[:, col : col + P], words[:, u : K // 2 : 2], ident[:])
            dst = held["grouped", m, load][:].bitcast(F32)[:, half * BANK : (half + 1) * BANK]
            nc.scalar.copy(
                out=dst.rearrange("p (i r u) -> p i r u", i=2, u=2),
                in_=bank[:].rearrange("p (i u r) -> p i r u", i=2, u=2),
            )

        def quantize_input(m, load):
            codes = work.tile([P, BANK], U32, name="row_codes%d" % m, bufs=4, align_bytes=64)
            scales = work.tile([P, BANK], U8, name="row_scales%d" % m, bufs=4, align_bytes=64)
            nc.vector.quantize_mx(out=codes[:].bitcast(FP8X4), scales=scales[:], in_=held["grouped", m, load][:])
            held["codes", m, load] = (codes, scales)

        def product_rows(bank, m, g, t, c):
            codes, scales = held["codes", m, g // PER_LOAD]
            first = g % PER_LOAD * ROWS + t * P
            rows, cols = slice(first, first + P), slice(c * BANK, (c + 1) * BANK)
            nc.tensor.matmul_mx(
                out=bank,
                lhsT=codes[:, rows].bitcast(FP8X4),
                lhsT_scale=scales[:, rows],
                rhs=w_codes[m][:, cols].bitcast(FP8X4),
                rhs_scale=w_scales[m][:, cols],
                start=True,
                stop=True,
            )

        def product_channels(out, m, g, j):
            codes, scales = held["codes", m, g // PER_LOAD]
            first = g % PER_LOAD * ROWS
            rows, cols = slice(first, first + ROWS), slice(j * P, (j + 1) * P)
            nc.tensor.matmul_mx(
                out=out,
                lhsT=w_codes[m][:, cols].bitcast(FP8X4),
                lhsT_scale=w_scales[m][:, cols],
                rhs=codes[:, rows].bitcast(FP8X4),
                rhs_scale=scales[:, rows],
                start=True,
                stop=True,
            )

        def open_stats(g):
            held["mean_var", g] = work.tile([P, PAIRS, 2], F32, name="mean_var", bufs=6)
            held["squares", g] = work.tile([P, TILES, 2], F32, name="squares", bufs=3)

        def vector_stats(g, pair, c):
            if ("bn", g, pair) not in held:
                held["bn", g, pair] = work.tile([P, CHUNKS, 6], F32, name="bn", bufs=2 * PAIRS)
            bank = vector_bank()
            product_rows(bank[:], pair // TILES, g, pair % TILES, c)
            nc.vector.bn_stats(out=held["bn", g, pair][:, c, :], in_=bank[:])

        def vector_stats_end(g, pair):
            parts = held["bn", g, pair][:].rearrange("p c s -> p (c s)")
            nc.vector.bn_aggr(out=held["mean_var", g][:, pair, :], in_=parts)

        def scalar_sum(g, pair, c):
            if c == 0:
                held["scaled", g, pair] = work.tile([P, G], F32, name="scaled")
                held["part", g, pair] = work.tile([P, 2, CHUNKS], F32, name="part", bufs=3)
            bank = scalar_bank()
            product_rows(bank[:], pair // TILES, g, pair % TILES, c)
            nc.scalar.activation(
                out=held["scaled", g, pair][:, c * BANK : (c + 1) * BANK],
                in_=bank[:],
                func=ACT.Copy,
                scale=1.0 / G,
                accum_out=held["part", g, pair][:, 0, c : c + 1],
            )

        def scalar_mean(g, pair):
            part = held["part", g, pair]
            mean = held["mean_var", g][:, pair, 0:1]
            nc.scalar.activation(out=part[:, 1, :], in_=part[:, 0, :], func=ACT.Copy, accum_out=mean)

        def scalar_squares(g, pair, half):
            scaled = held["scaled", g, pair][:, half * G // 2 : (half + 1) * G // 2]
            nc.scalar.activation(
                out=scaled,
                in_=scaled,
                func=ACT.Square,
                scale=-float(G),
                bias=held["mean_var", g][:, pair, 0:1],
                accum_out=held["squares", g][:, pair % TILES, half : half + 1],
            )

        def scalar_var(g, pair):
            halves = held["squares", g][:, pair % TILES, :]
            var = held["mean_var", g][:, pair, 1:2]
            nc.scalar.activation(out=halves, in_=halves, func=ACT.Copy, scale=1.0 / G, accum_out=var)

        def row_rstd(g):
            mean_var = held["mean_var", g]
            var_eps = work.tile([P, PAIRS], F32, name="var_eps", bufs=5)
            rstd = work.tile([P, PAIRS], F32, name="rstd", bufs=5)
            terms = work.tile([P, PAIRS, TERMS], F32, name="terms", bufs=5)
            nc.gpsimd.tensor_scalar(var_eps[:], mean_var[:, :, 1], 1.0, EPS, ALU.mult, ALU.add)
            nc.gpsimd.tensor_tensor(rstd[:], var_eps[:], minus_half[:], ALU.pow)
            nc.gpsimd.tensor_scalar(terms[:, :, 2], mean_var[:, :, 0], -1.0, 0.0, ALU.mult, ALU.add)
            held["rstd", g], held["var_eps", g], held["terms", g] = rstd, var_eps, terms

        def row_std(g):
            twice = [P, TILES, 2]
            nc.gpsimd.tensor_tensor(
                held["terms", g][:, :TILES, 0:2],
                held["var_eps", g][:, :TILES].unsqueeze(2).to_broadcast(twice),
                held["rstd", g][:, :TILES].unsqueeze(2).to_broadcast(twice),
                ALU.mult,
            )

        def row_ratio(g):
            ratio = work.tile([P, TILES], F32, name="ratio", bufs=5)
            nc.gpsimd.tensor_tensor(ratio[:], held["terms", g][:, :TILES, 0], held["rstd", g][:, TILES:], ALU.mult)
            held["ratio", g] = ratio

        def row_mean_hh(g):
            terms = held["terms", g]
            nc.gpsimd.tensor_tensor(terms[:, :TILES, 3], terms[:, TILES:, 2], held["ratio", g][:], ALU.mult)
            held["rest", g] = terms[:, :TILES, :]

        def piece_view(g, i):
            used = pieces[g % 2][:, :, : TERMS * PIECES]
            return used.rearrange("p t (v s) -> p t v s", s=PIECES)[:, :, :, i]

        def row_piece(g, i):
            nc.gpsimd.tensor_copy(out=piece_view(g, i), in_=held["rest", g])

        def row_rest(g, i):
            rest = work.tile([P, TILES, TERMS], F32, name="rest", bufs=4)
            nc.gpsimd.tensor_tensor(rest[:], held["rest", g], piece_view(g, i), ALU.subtract)
            held["rest", g] = rest[:]

        factor_chain = [(row_std,), (row_ratio,), (row_mean_hh,)]
        factor_chain += [(row_piece, 0), (row_rest, 0), (row_piece, 1), (row_rest, 1), (row_piece, 2)]

        def spread_ratio(g):
            bank = scalar_bank()
            for t in range(TILES):
                repeated = held["ratio", g][:, t : t + 1].to_broadcast([P, P])
                nc.tensor.transpose(bank[:, t * P : (t + 1) * P], repeated, ident[:])
            ratio_all = work.tile([P, ROWS], F32, name="ratio_all")
            nc.scalar.copy(out=ratio_all[:], in_=bank[:, :ROWS])
            held["ratio_all", g] = ratio_all

        def turn_pieces(g):
            bank = scalar_bank(BF16)
            for t in range(TILES):
                nc.tensor.transpose(bank[:, t * P : (t + 1) * P], pieces[g % 2][:, t, :], ident_bf[:])
            shift_lhs = work.tile([P, ROWS], BF16, name="shift_lhs")
            nc.scalar.copy(out=shift_lhs[:], in_=bank[:, :ROWS])
            held["shift_lhs", g] = shift_lhs

        def channel_products(bank, m, g, s):
            found = []
            for i in range(PER_BANK):
                q, block = divmod(s * PER_BANK + i, BLOCKS)
                j = GATE_ORDER[q] * BLOCKS + block
                cols = bank[:, i * ROWS : (i + 1) * ROWS]
                product_channels(cols, m, g, j)
                found.append((cols, gain_cols[:, m * G // P + j : m * G // P + j + 1]))
            return found

        def scaled_tile(m):
            return work.tile([P, PER_BANK, ROWS], F32, name="gained%d" % m, bufs=5)

        def gained_ih(g, s):
            gained = scaled_tile(IH)
            for i, (cols, gamma) in enumerate(channel_products(scalar_bank(), IH, g, s)):
                nc.scalar.activation(out=gained[:, i, :], in_=cols, func=ACT.Copy, scale=gamma)
            held["gained", IH, g, s] = gained

        def gained_hh(g, s):
            gained = scaled_tile(HH)
            for i, (cols, gamma) in enumerate(channel_products(vector_bank(), HH, g, s)):
                nc.vector.scalar_tensor_tensor(
                    gained[:, i, :], cols, gamma, held["ratio_all", g][:], ALU.mult, ALU.mult
                )
            held["gained", HH, g, s] = gained

        def gate_tile(which):
            return work.tile([P, H], F32, name="gate%d" % which, bufs=7 if which == GATE_O else 4)

        def gate(g, item):
            q, t = divmod(item, TILES)
            which = GATE_ORDER[q]
            rows = slice(t * P, (t + 1) * P)
            bank = scalar_bank()
            nc.tensor.matmul(
                bank[:],
                held["shift_lhs", g][:, rows],
                shift_rhs[:, which * H : (which + 1) * H],
                start=True,
                stop=False,
            )
            for m in (IH, HH):
                for i in range(BLOCKS):
                    s, slot = divmod(BLOCKS * q + i, PER_BANK)
                    nc.tensor.matmul(
                        bank[:, i * P : (i + 1) * P],
                        held["gained", m, g, s][:, slot, rows],
                        ident[:],
                        start=False,
                        stop=(m == HH and i == BLOCKS - 1),
                        is_transpose=True,
                    )
            value = gate_tile(which)
            func = ACT.Tanh if which == GATE_G else ACT.Sigmoid
            nc.scalar.activation(out=value[:], in_=bank[:], func=func, scale=held["rstd", g][:, t : t + 1])
            held["gate", which, g, t] = value

        def o_centred(g, t, m):
            bank = vector_bank()
            product_rows(bank[:], m, g, t, GATE_O)
            part = work.tile([P, H], F32, name="o_part%d" % m, bufs=3)
            mean = held["mean_var", g][:, m * TILES + t, 0:1]
            nc.vector.scalar_tensor_tensor(part[:], bank[:], mean, gamma_o[m][:], ALU.subtract, ALU.mult)
            held["o_part", m, g, t] = part

        def o_sum(g, t):
            total, ratio = held["o_part", HH, g, t], held["ratio", g][:, t : t + 1]
            nc.vector.scalar_tensor_tensor(total[:], total[:], ratio, held["o_part", IH, g, t][:], ALU.mult, ALU.add)

        def o_bias(g, t):
            total, std = held["o_part", HH, g, t], held["terms", g][:, t, 0:1]
            nc.vector.scalar_tensor_tensor(total[:], beta_o[:], std, total[:], ALU.mult, ALU.add)

        def o_gate(g, t):
            value = gate_tile(GATE_O)
            rstd = held["rstd", g][:, t : t + 1]
            nc.scalar.activation(out=value[:], in_=held["o_part", HH, g, t][:], func=ACT.Sigmoid, scale=rstd)
            held["gate", GATE_O, g, t] = value

        def cell_engine(g):
            return nc.vector if g == LAST else nc.gpsimd

        def tile_rows(g, t):
            return slice((g * TILES + t) * P, (g * TILES + t + 1) * P)

        def input_term(g, t):
            i_gate = held["gate", GATE_I, g, t]
            cell_engine(g).tensor_tensor(i_gate[:], i_gate[:], held["gate", GATE_G, g, t][:], ALU.mult)

        def forget_term(g, t):
            f_gate = held["gate", GATE_F, g, t]
            c_old = held["c_prev", g // PER_LOAD][:, g % PER_LOAD * TILES + t, :]
            cell_engine(g).tensor_tensor(f_gate[:], f_gate[:], c_old, ALU.mult)

        def cell_sum(g, t):
            c_new = work.tile([P, H], F32, name="c_new", bufs=4)
            terms = held["gate", GATE_F, g, t], held["gate", GATE_I, g, t]
            cell_engine(g).tensor_tensor(c_new[:], terms[0][:], terms[1][:], ALU.add)
            nc.sync.dma_start(out=out_1[tile_rows(g, t), :], in_=c_new[:])
            held["c", g, t] = c_new

        def cell_stats(g, t):
            bn = work.tile([P, 6], F32, name="c_bn")
            nc.vector.bn_stats(out=bn[:], in_=held["c", g, t][:])
            held["c_bn", g, t] = bn

        def cell_mean(g, t):
            mean_var = work.tile([P, 2], F32, name="c_mean_var", bufs=3)
            nc.vector.bn_aggr(out=mean_var[:], in_=held["c_bn", g, t][:])
            held["c_mean_var", g, t] = mean_var

        def cell_var(g, t):
            var_eps = work.tile([P, 1], F32, name="c_var_eps", bufs=3)
            nc.gpsimd.tensor_scalar(var_eps[:], held["c_mean_var", g, t][:, 1:2], 1.0, EPS, ALU.mult, ALU.add)
            held["c_var_eps", g, t] = var_eps

        def cell_rstd(g, t):
            rstd = work.tile([P, 1], F32, name="c_rstd", bufs=3)
            nc.gpsimd.tensor_tensor(rstd[:], held["c_var_eps", g, t][:], minus_half[:, 0:1], ALU.pow)
            held["c_rstd", g, t] = rstd

        def cell_rstd_at_once(g, t):
            cell_rstd(g, t)

        def cell_normed(g, t):
            normed = work.tile([P, H], F32, name="c_normed", bufs=4)
            mean, rstd = held["c_mean_var", g, t][:, 0:1], held["c_rstd", g, t][:]
            nc.vector.tensor_scalar(normed[:], held["c", g, t][:], mean, rstd, ALU.subtract, ALU.mult)
            held["c_normed", g, t] = normed

        def turn_tile(bank, src):
            for i in range(BLOCKS):
                nc.tensor.transpose(bank[:, i * P : (i + 1) * P], src[:, i * P : (i + 1) * P], ident[:])

        def cell_tanh(g, t):
            bank = scalar_bank()
            turn_tile(bank, held["c_normed", g, t])
            c_tanh = work.tile([P, H], F32, name="c_tanh", bufs=4)
            for i in range(BLOCKS):
                nc.scalar.activation(
                    out=c_tanh[:, i * P : (i + 1) * P],
                    in_=bank[:, i * P : (i + 1) * P],
                    func=ACT.Tanh,
                    scale=gain_cols[:, NORM_COL + i : NORM_COL + i + 1],
                    bias=gain_cols[:, NORM_COL + BLOCKS + i : NORM_COL + BLOCKS + i + 1],
                )
            held["c_tanh", g, t] = c_tanh

        def hidden(g, t):
            bank = vector_bank()
            turn_tile(bank, held["c_tanh", g, t])
            h_new = work.tile([P, H], F32, name="h_new", bufs=3)
            nc.vector.tensor_tensor(h_new[:], bank[:], held["gate", GATE_O, g, t][:], ALU.mult)
            nc.sync.dma_start(out=out_0[tile_rows(g, t), :], in_=h_new[:])

        def head_stats(m, c):
            for t in range(TILES):
                vector_stats(0, m * TILES + t, c)

        load_weight(IH, 0)
        load_input(IH, 0)
        load_weight(IH, 1)
        load_weight(IH, 2)
        load_input(HH, 0)
        load_weight(IH, 3)
        make_identity(nc, ident[:])
        make_identity(nc, ident_bf[:])
        nc.gpsimd.memset(gain_rows[:], 0.0)
        nc.gpsimd.memset(shift_rhs[:], 0.0)
        nc.gpsimd.memset(minus_half[:], -0.5)
        for tile in pieces:
            nc.gpsimd.memset(tile[:], 0.0)
        open_stats(0)

        interleave_weight(IH, 0, nc.vector.tensor_copy)
        load_weight(HH, 0)
        turn_input(IH, 0, 0)
        turn_input(IH, 0, 1)
        load_weight(HH, 1)
        quantize_weight(IH, 0)
        interleave_weight(IH, 1, nc.scalar.copy)
        load_weight(HH, 2)
        quantize_input(IH, 0)
        interleave_weight(IH, 2, nc.vector.tensor_copy)
        load_weight(HH, 3)
        vector_stats(0, 0, 0)
        quantize_weight(IH, 2)
        quantize_weight(IH, 1)
        turn_input(HH, 0, 0)
        turn_input(HH, 0, 1)
        load_input(IH, 1)
        vector_stats(0, 1, 0)
        head_stats(IH, 2)
        quantize_input(HH, 0)
        interleave_weight(IH, 3, nc.scalar.copy)
        load_input(HH, 1)
        interleave_weight(HH, 0, nc.vector.tensor_copy)
        vector_stats(0, 0, 1)
        quantize_weight(HH, 0)
        quantize_weight(IH, 3)
        interleave_weight(HH, 1, nc.scalar.copy)
        interleave_weight(HH, 2, nc.vector.tensor_copy)
        vector_stats(0, 1, 1)
        quantize_weight(HH, 2)
        quantize_weight(HH, 1)
        interleave_weight(HH, 3, nc.scalar.copy)
        head_stats(IH, 3)
        head_stats(HH, 0)
        quantize_weight(HH, 3)

        row = 0
        for vec in (gamma_ih, gamma_hh, gamma_c, beta_c):
            blocks = vec.shape[0] // P
            nc.sync.dma_start(out=gain_rows[row : row + blocks, :], in_=vec.rearrange("(j n) -> j n", n=P))
            row += blocks
        for v, vec in enumerate((beta_ih, beta_hh, gamma_ih, gamma_hh)):
            nc.sync.dma_start(out=shift_rhs[PIECES * v : PIECES * (v + 1), :], in_=vec.partition_broadcast(PIECES))
        for dst, vec in zip(gamma_o + beta_o_parts, (gamma_ih, gamma_hh, beta_ih, beta_hh)):
            nc.sync.dma_start(out=dst[:], in_=vec[GATE_O * H :].partition_broadcast(P))
        nc.gpsimd.tensor_tensor(beta_o[:], beta_o_parts[IH][:], beta_o_parts[HH][:], ALU.add)
        gain_bank = scalar_bank(BF16)
        nc.tensor.transpose(gain_bank[:, :P], gain_rows[:], ident_bf[:])
        nc.scalar.copy(out=gain_cols[:], in_=gain_bank[:, : NORM_COL + 2 * BLOCKS])

        for_vector = (gained_hh, o_centred, vector_stats)
        for_scalar = (gained_ih, scalar_sum)
        then = [open_stats, load_input, cell_stats, o_gate, scalar_var, scalar_squares]
        then += [input_term, forget_term, cell_sum, cell_rstd, o_sum, cell_normed, o_bias, cell_mean, cell_var]
        then += [cell_rstd_at_once, load_cell, quantize_input, vector_stats_end, scalar_mean, row_rstd]
        then += [entry[0] for entry in factor_chain[:5]]
        then += [gate, spread_ratio, turn_pieces, turn_input, cell_tanh, hidden]
        factor_rank = then.index(row_std)
        whole_passes = (gained_hh, o_centred, o_sum, o_bias, cell_stats, hidden, quantize_input, vector_stats)
        vector_passes = {fn: 1 for fn in whole_passes}
        vector_passes[cell_normed] = 0.5
        plan = {}
        ending = {}

        def at(step, fn, *args):
            plan.setdefault(step, []).append((fn, args))

        def passes(step):
            return sum(vector_passes.get(fn, 0) for fn, args in plan.get(step, []))

        for c in range(1, CHUNKS):
            for t in range(TILES):
                at(0, vector_stats, 0, HH * TILES + t, c)
        for pair in range(PAIRS):
            at(0, vector_stats_end, 0, pair)
        at(0, row_rstd, 0)
        for link in factor_chain:
            at(1, link[0], 0, *link[1:])

        for g in range(GROUPS):
            base = PERIOD * g + FIRST
            if g > 0:
                at(base - FACTOR_LEAD, row_rstd, g)
                for n, link in enumerate(factor_chain):
                    at(base - FACTOR_LEAD + n // 2, link[0], g, *link[1:])
            at(base - 2 if g > 0 else base - 1, spread_ratio, g)
            at(base + 1, turn_pieces, g)
            if g % PER_LOAD == 0:
                at(base, load_cell, g // PER_LOAD)
            for s in range(PERIOD + TILES if g == LAST else PERIOD):
                at(base + s, gained_hh, g, s)
                at(base + s, gained_ih, g, s)
                at(base + s + TILES, gate, g, s)
            if g == LAST:
                continue
            for t in range(TILES):
                done = base + PERIOD + TILE_GAP * t
                for fn in (input_term, forget_term, cell_sum):
                    at(done + 1, fn, g, t)
                for fn in (cell_stats, cell_mean, cell_var):
                    at(done + TILE_GAP, fn, g, t)
                if (g, t) == (LAST - 1, TILES - 1):
                    at(done + TILE_GAP, cell_rstd_at_once, g, t)
                    normed_at = done + TILE_GAP + 1
                else:
                    at(done + TILE_GAP + 1, cell_rstd, g, t)
                    normed_at = done + 2 * TILE_GAP
                for n, fn in enumerate((cell_normed, cell_tanh, hidden)):
                    at(normed_at + n, fn, g, t)
                o_at = base + TILE_GAP * (t + 1)
                at(o_at - 1, o_centred, g, t, IH)
                at(o_at - 1, o_centred, g, t, HH)
                at(o_at, o_sum, g, t)
                at(o_at, o_bias, g, t)
                at(o_at + 1, o_gate, g, t)

        f_done = PERIOD * LAST + FIRST + PERIOD
        for t in range(TILES):
            at(f_done - 1 + t, input_term, LAST, t)
        ending[f_done] = [(fn, 0) for fn in (forget_term, cell_sum, cell_stats, cell_mean, cell_var, cell_rstd)]
        ending[f_done + 1] = [(forget_term, 1), (cell_normed, 0)]
        ending[f_done + 1] += [(fn, 1) for fn in (cell_sum, cell_stats, cell_mean, cell_var, cell_rstd)]
        ending[f_done + 2] = [(cell_normed, 1), (cell_tanh, 0), (hidden, 0)]
        ending[f_done + 3] = [(cell_tanh, 1), (hidden, 1)]

        ready = {0: 0}
        for load in range(1, B // (LOAD_TILES * P)):
            begin = 4 * (load - 1)
            for m in (IH, HH):
                if load > 1:
                    at(begin - 4, load_input, m, load)
                at(begin + 2 * m, turn_input, m, load, 0)
                at(begin + 2 * m + 1, turn_input, m, load, 1)
                at(begin + 2 * m + 2, quantize_input, m, load)
            ready[load] = begin + 5

        opened = {}
        vector_work = []
        free = 0
        for g in range(1, GROUPS):
            free = max(free, ready[g // PER_LOAD])
            opened[g] = free
            taken = min(TILES, (PERIOD * g + FIRST - FACTOR_LEAD - free) // SCALAR_SPAN)
            for pair in range(PAIRS - taken, PAIRS):
                for c in range(CHUNKS):
                    at(free + c // 2, scalar_sum, g, pair, c)
                at(free + 1, scalar_mean, g, pair)
                at(free + 2, scalar_squares, g, pair, 0)
                at(free + 3, scalar_squares, g, pair, 1)
                at(free + SCALAR_SPAN, scalar_var, g, pair)
                free += SCALAR_SPAN
            vector_work += [(g, pair, c) for pair in range(PAIRS - taken) for c in range(CHUNKS)]
        stats_steps = range(1, PERIOD * LAST + FIRST - FACTOR_LEAD)
        total = len(vector_work) + sum(passes(step) for step in stats_steps)
        spent = 0
        placed = 0
        for step in stats_steps:
            spent += passes(step)
            while placed < len(vector_work):
                g, pair, c = vector_work[placed]
                due = PERIOD * g + FIRST - FACTOR_LEAD - 1
                ahead = spent >= total * step // len(stats_steps)
                if (ahead and step < due) or step < ready[g // PER_LOAD]:
                    break
                opened[g] = min(opened[g], step)
                at(step, vector_stats, g, pair, c)
                if c == CHUNKS - 1:
                    at(step, vector_stats_end, g, pair)
                placed += 1
                spent += 1
        for g in range(1, GROUPS):
            at(opened[g] - 1, open_stats, g)

        for step in sorted(plan):
            vector_banks = [e for e in plan[step] if e[0] in for_vector]
            scalar_banks = [e for e in plan[step] if e[0] in for_scalar]
            order = []
            for i in range(max(len(vector_banks), len(scalar_banks))):
                order += vector_banks[i : i + 1] + scalar_banks[i : i + 1]
            others = [e for e in plan[step] if e[0] in then]
            chained = [entry[0] for entry in factor_chain]
            order += sorted(others, key=lambda e: factor_rank if e[0] in chained else then.index(e[0]))
            for fn, args in order:
                fn(*args)
            for fn, t in ending.get(step, []):
                fn(LAST, t)
